import numpy as np
import ml_dtypes


def mxq(x, axis, fmt="e4m3"):
    dtype, down = {"e4m3": (ml_dtypes.float8_e4m3fn, 7), "e5m2": (ml_dtypes.float8_e5m2, 14)}[fmt]
    v = np.moveaxis(np.asarray(x, np.float32).astype(ml_dtypes.bfloat16).astype(np.float64), axis, -1)
    blocks = v.reshape(v.shape[:-1] + (-1, 32))
    amax = np.abs(blocks).max(-1, keepdims=True)
    byte = np.maximum(np.where(amax > 0, np.frexp(amax)[1] - 1 + 127, 0) - down, 1)
    scale = np.exp2(byte - 127.0)
    codes = (blocks / scale).astype(np.float32).astype(dtype).astype(np.float64)
    return np.moveaxis((codes * scale).reshape(v.shape), -1, axis)


BF16 = ml_dtypes.bfloat16


def bf(x):
    return np.asarray(x, np.float32).astype(BF16)


def f64(x):
    return np.asarray(x).astype(np.float64)


B, T, H, HD, C = 2, 1024, 8, 128, 64
P = 8


def sigmoid(v):
    return 1.0 / (1.0 + np.exp(-v))


def palace_mask(w):
    idx = np.arange(T) % P
    intra = idx[:, None] == idx[None, :]
    return np.where(intra, 1.0, sigmoid(w))


def setup_inputs():
    c = np.repeat(np.random.standard_normal((B, T // C, H * HD)), C, axis=1)
    z = np.random.standard_normal((B, T, H * HD))
    x = np.sqrt(6.0 / np.sqrt(HD)) * c + np.sqrt(2.0 / np.sqrt(HD)) * z
    return {"x": bf(x), "inter_palace_weight": bf(0.6 + 0.2 * np.random.standard_normal(1))}


def reference(x, inter_palace_weight):
    q = f64(x).reshape(B, T, H, HD).transpose(0, 2, 1, 3)
    scores = (q @ q.transpose(0, 1, 3, 2)) * HD ** -0.5
    s = scores * palace_mask(f64(inter_palace_weight))
    e = np.exp(s - s.max(-1, keepdims=True))
    out = (mxq(e, 3, "e4m3") @ mxq(q, 2, "e4m3")) / e.sum(-1, keepdims=True)
    return out.transpose(0, 2, 1, 3).reshape(B, T, H * HD)

@@ -1,0 +1,234 @@
+from contextlib import ExitStack
+
+import concourse.mybir as mybir
+from concourse.masks import make_identity
+
+FP32 = mybir.dt.float32
+BF16 = mybir.dt.bfloat16
+U32 = mybir.dt.uint32
+U8 = mybir.dt.uint8
+FP8X4 = mybir.dt.float8_e4m3fn_x4
+ALU = mybir.AluOpType
+ACTF = mybir.ActivationFunctionType
+AXIS = mybir.AxisListType
+
+NB, T, H, HD = 2, 1024, 8, 128
+NPAL = 8
+P = 128
+NHEADS = NB * H
+NTILES = NHEADS * NPAL
+SCALE = HD ** -0.5
+FLOPS = 2 * 2 * NB * H * T * T * HD
+PINNED = True
+EVAC_ON_VECTOR = (6,)
+
+
+def tile_palaceattention_kernel(tc, x, inter_palace_weight, out):
+    nc = tc.nc
+    with ExitStack() as ctx:
+        const = ctx.enter_context(tc.tile_pool(name="const", bufs=1))
+        headp = ctx.enter_context(tc.tile_pool(name="headp", bufs=2))
+        work = ctx.enter_context(tc.tile_pool(name="work", bufs=3))
+        small = ctx.enter_context(tc.tile_pool(name="small", bufs=4))
+        ps_s = ctx.enter_context(tc.psum_pool(name="ps_s", bufs=2))
+        ps_x = ctx.enter_context(tc.psum_pool(name="ps_x", bufs=2))
+        ps_1 = ctx.enter_context(tc.psum_pool(name="ps_1", bufs=1))
+
+        xv = [x[b].rearrange("(a p) c -> a p c", p=NPAL) for b in range(NB)]
+        ov = [out[b].rearrange("(a p) c -> a p c", p=NPAL) for b in range(NB)]
+
+        w_bf = const.tile([P, 1], BF16)
+        nc.sync.dma_start(out=w_bf[:], in_=inter_palace_weight.partition_broadcast(P))
+        x0 = const.tile([P, NPAL, H * HD], BF16)
+        x1 = const.tile([P, NPAL, H * HD], BF16)
+        xin = [x0, x1]
+        for b in range(NB):
+            for c in range(4):
+                cols = slice(c * 256, (c + 1) * 256)
+                nc.sync.dma_start(out=xin[b][:, :, cols], in_=xv[b][:, :, cols])
+
+        ident = const.tile([P, P], BF16)
+        make_identity(nc, ident[:])
+        sig = const.tile([P, 1], FP32)
+        nc.scalar.activation(out=sig[:], in_=w_bf[:], func=ACTF.Sigmoid)
+        csig = const.tile([P, 1], FP32)
+        nc.vector.tensor_scalar(out=csig[:], in0=sig[:], scalar1=SCALE, scalar2=None, op0=ALU.mult)
+
+        st = {}
+
+        def prep_transposes(hh):
+            b, h = divmod(hh, H)
+            pt = ps_1.tile([P, NPAL, P], BF16, tag="pt")
+            for pal in range(NPAL):
+                nc.tensor.transpose(pt[:, pal, :], xin[b][:, pal, h * HD:(h + 1) * HD], ident[:])
+            st[("pt", hh)] = pt
+
+        def prep_copy(hh):
+            qt = headp.tile([P, NPAL * P], BF16, tag="qt")
+            nc.vector.tensor_copy(out=qt[:], in_=st[("pt", hh)][:].rearrange("p a q -> p (a q)"))
+            st[("qt", hh)] = qt
+
+        def prep_regroup(hh):
+            b, h = divmod(hh, H)
+            qg = headp.tile([P, 2, HD, 4], BF16, tag="qg", align_bytes=64)
+            src = xin[b][:, :, h * HD:(h + 1) * HD].rearrange("p (g t) d -> p g d t", t=4)
+            nc.vector.tensor_copy(out=qg[:], in_=src)
+            st[("qg", hh)] = qg
+
+        def prep_quant(hh):
+            qc = headp.tile([P, 2 * HD], U32, tag="qc", align_bytes=64)
+            qs = headp.tile([P, 2 * HD], U8, tag="qs", align_bytes=64)
+            nc.vector.quantize_mx(
+                out=qc[:].bitcast(FP8X4),
+                scales=qs[:],
+                in_=st[("qg", hh)][:].rearrange("p g d t -> p (g d t)"),
+            )
+            st[("qc", hh)] = qc
+            st[("qs", hh)] = qs
+
+        def qk(i):
+            hh, pq = divmod(i, NPAL)
+            qt = st[("qt", hh)]
+            lhs = qt[:, pq * P:(pq + 1) * P]
+            s_a = ps_s.tile([P, 512], FP32, tag="s_a")
+            s_b = ps_s.tile([P, 512], FP32, tag="s_b")
+            for bank, dst in ((0, s_a), (1, s_b)):
+                first = (pq + 4 * bank) % NPAL
+                n1 = min(4, NPAL - first)
+                nc.tensor.matmul(dst[:, 0:n1 * P], lhsT=lhs, rhs=qt[:, first * P:(first + n1) * P],
+                                 start=True, stop=True)
+                if n1 < 4:
+                    nc.tensor.matmul(dst[:, n1 * P:512], lhsT=lhs, rhs=qt[:, 0:(4 - n1) * P],
+                                     start=True, stop=True)
+            st[("s", i)] = (s_a, s_b)
+
+        def pass_main(i):
+            s_a, s_b = st[("s", i)]
+            sm = work.tile([P, T], FP32, tag="sm")
+            mx = small.tile([P, 4], FP32, tag="mx")
+            nc.vector.tensor_scalar(out=sm[:, 0:P], in0=s_a[:, 0:P], scalar1=SCALE, scalar2=None,
+                                    op0=ALU.mult, op1=ALU.max, accum_out=mx[:, 0:1])
+            nc.vector.tensor_scalar(out=sm[:, P:512], in0=s_a[:, P:512], scalar1=csig[:, 0:1], scalar2=None,
+                                    op0=ALU.mult, op1=ALU.max, accum_out=mx[:, 1:2])
+            nc.vector.tensor_scalar(out=sm[:, 512:T], in0=s_b[:], scalar1=csig[:, 0:1], scalar2=None,
+                                    op0=ALU.mult, op1=ALU.max, accum_out=mx[:, 2:3])
+            st[("sm", i)] = sm
+            st[("mx", i)] = mx
+
+        def pass_fin(i):
+            nb = small.tile([P, 1], FP32, tag="nb")
+            nc.vector.tensor_reduce(out=nb[:], in_=st[("mx", i)][:, 0:3], axis=AXIS.X, op=ALU.max, negate=True)
+            st[("nb", i)] = nb
+
+        def expo(i):
+            j, k = divmod(i, 4)
+            if k == 0:
+                rs = small.tile([P, 4], FP32, tag="rs")
+                st[("rs", j)] = rs
+            e = work.tile([P, T], BF16, tag="e")
+            nc.scalar.activation(out=e[:], in_=st[("sm", i)][:], func=ACTF.Exp, bias=st[("nb", i)][:, 0:1],
+                                 scale=1.0, accum_out=st[("rs", j)][:, k:k + 1])
+            st[("e", i)] = e
+
+        def transposes(i):
+            pq = i % NPAL
+            e = st[("e", i)]
+            xt = ps_x.tile([P, NPAL, P], BF16, tag="xt")
+            for k in range(NPAL):
+                nc.tensor.transpose(xt[:, (pq + k) % NPAL, :], e[:, k * P:(k + 1) * P], ident[:])
+            st[("xt", i)] = xt
+
+        def evac(i):
+            gr = work.tile([P, 2, P, 4], BF16, tag="gr", align_bytes=64)
+            src = st[("xt", i)][:].rearrange("p (g t) q -> p g q t", t=4)
+            if i % NPAL in EVAC_ON_VECTOR:
+                nc.vector.tensor_copy(out=gr[:], in_=src)
+            else:
+                nc.scalar.copy(out=gr[:], in_=src)
+            st[("gr", i)] = gr
+
+        def quant(i):
+            ec = work.tile([P, 2 * P], U32, tag="ec", align_bytes=64)
+            es = work.tile([P, 2 * P], U8, tag="es", align_bytes=64)
+            nc.vector.quantize_mx(
+                out=ec[:].bitcast(FP8X4),
+                scales=es[:],
+                in_=st[("gr", i)][:].rearrange("p g q t -> p (g q t)"),
+            )
+            st[("ec", i)] = ec
+            st[("es", i)] = es
+
+        def mx_matmul(i):
+            hh = i // NPAL
+            j, k = divmod(i, 4)
+            if k == 0:
+                o_ps = ps_1.tile([P, 4, HD], FP32, tag="o_ps")
+                st[("o_ps", j)] = o_ps
+            ec, es = st[("ec", i)], st[("es", i)]
+            qc, qs = st[("qc", hh)], st[("qs", hh)]
+            for g in range(2):
+                cols = slice(g * P, (g + 1) * P)
+                nc.tensor.matmul_mx(
+                    out=st[("o_ps", j)][:, k, :],
+                    lhsT=ec[:, cols].bitcast(FP8X4),
+                    lhsT_scale=es[:, cols],
+                    rhs=qc[:, cols].bitcast(FP8X4),
+                    rhs_scale=qs[:, cols],
+                    start=(g == 0),
+                    stop=(g == 1),
+                )
+
+        def norm(j):
+            hh, half = divmod(j, 2)
+            b, h = divmod(hh, H)
+            rinv = small.tile([P, 4], FP32, tag="rinv")
+            nc.vector.reciprocal(out=rinv[:], in_=st[("rs", j)][:])
+            o_sb = work.tile([P, 4, HD], FP32, tag="o_sb")
+            nc.vector.tensor_tensor(out=o_sb[:], in0=st[("o_ps", j)][:],
+                                    in1=rinv[:].unsqueeze(2).to_broadcast([P, 4, HD]), op=ALU.mult)
+            nc.sync.dma_start(out=ov[b][:, half * 4:(half + 1) * 4, h * HD:(h + 1) * HD], in_=o_sb[:])
+
+        def ok(i):
+            return 0 <= i < NTILES
+
+        def body():
+            prep_transposes(0)
+            prep_copy(0)
+            prep_regroup(0)
+            prep_quant(0)
+            for s in range(-2, NTILES + 4):
+                hh, r = divmod(s, NPAL)
+                nxt = hh + 1
+                if ok(s + 2):
+                    qk(s + 2)
+                if ok(s + 1):
+                    pass_main(s + 1)
+                if ok(s - 1):
+                    transposes(s - 1)
+                if 0 <= s and nxt < NHEADS and r == 1:
+                    prep_transposes(nxt)
+                if ok(s):
+                    expo(s)
+                if ok(s - 2):
+                    quant(s - 2)
+                if ok(s + 1):
+                    pass_fin(s + 1)
+                if ok(s - 1):
+                    evac(s - 1)
+                if 0 <= s and nxt < NHEADS:
+                    if r == 2:
+                        prep_copy(nxt)
+                    if r == 3:
+                        prep_regroup(nxt)
+                    if r == 4:
+                        prep_quant(nxt)
+                if ok(s - 3):
+                    mx_matmul(s - 3)
+                    if (s - 3) % 4 == 3:
+                        norm((s - 3) // 4)
+
+        if PINNED:
+            with tc.manual_schedule():
+                body()
+        else:
+            body()

@@ -20,7 +20,7 @@ NTILES = NHEADS * NPAL
 SCALE = HD ** -0.5
 FLOPS = 2 * 2 * NB * H * T * T * HD
 PINNED = True
-EVAC_ON_VECTOR = (6,)
+EVAC_ON_VECTOR = (2, 6)
 
 
 def tile_palaceattention_kernel(tc, x, inter_palace_weight, out):

@@ -17,10 +17,13 @@ NPAL = 8
 P = 128
 NHEADS = NB * H
 NTILES = NHEADS * NPAL
+NQUADS = NTILES // 4
 SCALE = HD ** -0.5
 FLOPS = 2 * 2 * NB * H * T * T * HD
 PINNED = True
-EVAC_ON_VECTOR = (2, 6)
+DIRECT = (3,)
+LEAD = 2
+GR_BUFS = 1
 
 
 def tile_palaceattention_kernel(tc, x, inter_palace_weight, out):
@@ -29,7 +32,8 @@ def tile_palaceattention_kernel(tc, x, inter_palace_weight, out):
         const = ctx.enter_context(tc.tile_pool(name="const", bufs=1))
         headp = ctx.enter_context(tc.tile_pool(name="headp", bufs=2))
         work = ctx.enter_context(tc.tile_pool(name="work", bufs=3))
-        small = ctx.enter_context(tc.tile_pool(name="small", bufs=4))
+        deep = ctx.enter_context(tc.tile_pool(name="deep", bufs=4))
+        grp = ctx.enter_context(tc.tile_pool(name="grp", bufs=GR_BUFS))
         ps_s = ctx.enter_context(tc.psum_pool(name="ps_s", bufs=2))
         ps_x = ctx.enter_context(tc.psum_pool(name="ps_x", bufs=2))
         ps_1 = ctx.enter_context(tc.psum_pool(name="ps_1", bufs=1))
@@ -65,14 +69,14 @@ def tile_palaceattention_kernel(tc, x, inter_palace_weight, out):
 
         def prep_copy(hh):
             qt = headp.tile([P, NPAL * P], BF16, tag="qt")
-            nc.vector.tensor_copy(out=qt[:], in_=st[("pt", hh)][:].rearrange("p a q -> p (a q)"))
+            nc.scalar.copy(out=qt[:], in_=st[("pt", hh)][:].rearrange("p a q -> p (a q)"))
             st[("qt", hh)] = qt
 
         def prep_regroup(hh):
             b, h = divmod(hh, H)
             qg = headp.tile([P, 2, HD, 4], BF16, tag="qg", align_bytes=64)
             src = xin[b][:, :, h * HD:(h + 1) * HD].rearrange("p (g t) d -> p g d t", t=4)
-            nc.vector.tensor_copy(out=qg[:], in_=src)
+            nc.gpsimd.tensor_scalar(out=qg[:], in0=src, scalar1=1.0, scalar2=0.0, op0=ALU.mult, op1=ALU.add)
             st[("qg", hh)] = qg
 
         def prep_quant(hh):
@@ -104,8 +108,8 @@ def tile_palaceattention_kernel(tc, x, inter_palace_weight, out):
 
         def pass_main(i):
             s_a, s_b = st[("s", i)]
-            sm = work.tile([P, T], FP32, tag="sm")
-            mx = small.tile([P, 4], FP32, tag="mx")
+            sm = deep.tile([P, T], FP32, tag="sm")
+            mx = deep.tile([P, 4], FP32, tag="mx")
             nc.vector.tensor_scalar(out=sm[:, 0:P], in0=s_a[:, 0:P], scalar1=SCALE, scalar2=None,
                                     op0=ALU.mult, op1=ALU.max, accum_out=mx[:, 0:1])
             nc.vector.tensor_scalar(out=sm[:, P:512], in0=s_a[:, P:512], scalar1=csig[:, 0:1], scalar2=None,
@@ -116,14 +120,14 @@ def tile_palaceattention_kernel(tc, x, inter_palace_weight, out):
             st[("mx", i)] = mx
 
         def pass_fin(i):
-            nb = small.tile([P, 1], FP32, tag="nb")
+            nb = deep.tile([P, 1], FP32, tag="nb")
             nc.vector.tensor_reduce(out=nb[:], in_=st[("mx", i)][:, 0:3], axis=AXIS.X, op=ALU.max, negate=True)
             st[("nb", i)] = nb
 
         def expo(i):
             j, k = divmod(i, 4)
             if k == 0:
-                rs = small.tile([P, 4], FP32, tag="rs")
+                rs = deep.tile([P, 4], FP32, tag="rs")
                 st[("rs", j)] = rs
             e = work.tile([P, T], BF16, tag="e")
             nc.scalar.activation(out=e[:], in_=st[("sm", i)][:], func=ACTF.Exp, bias=st[("nb", i)][:, 0:1],
@@ -139,49 +143,60 @@ def tile_palaceattention_kernel(tc, x, inter_palace_weight, out):
             st[("xt", i)] = xt
 
         def evac(i):
-            gr = work.tile([P, 2, P, 4], BF16, tag="gr", align_bytes=64)
-            src = st[("xt", i)][:].rearrange("p (g t) q -> p g q t", t=4)
-            if i % NPAL in EVAC_ON_VECTOR:
-                nc.vector.tensor_copy(out=gr[:], in_=src)
+            j, k = divmod(i, 4)
+            xt = st[("xt", i)]
+            if k in DIRECT:
+                nc.scalar.copy(out=st[("gr", j)][:, k], in_=xt[:].rearrange("p (g t) q -> p g q t", t=4))
             else:
-                nc.scalar.copy(out=gr[:], in_=src)
-            st[("gr", i)] = gr
+                tsb = deep.tile([P, NPAL, P], BF16, tag="tsb")
+                nc.scalar.copy(out=tsb[:].rearrange("p a q -> p (a q)"), in_=xt[:].rearrange("p a q -> p (a q)"))
+                st[("tsb", i)] = tsb
 
-        def quant(i):
-            ec = work.tile([P, 2 * P], U32, tag="ec", align_bytes=64)
-            es = work.tile([P, 2 * P], U8, tag="es", align_bytes=64)
+        def regroup(i):
+            j, k = divmod(i, 4)
+            if k == 0:
+                gr = grp.tile([P, 4, 2, P, 4], BF16, tag="gr", align_bytes=64)
+                st[("gr", j)] = gr
+            if k not in DIRECT:
+                nc.gpsimd.tensor_scalar(out=st[("gr", j)][:, k],
+                                        in0=st[("tsb", i)][:].rearrange("p (g t) q -> p g q t", t=4),
+                                        scalar1=1.0, scalar2=0.0, op0=ALU.mult, op1=ALU.add)
+
+        def quant(j):
+            ec = headp.tile([P, 8 * P], U32, tag="ec", align_bytes=64)
+            es = headp.tile([P, 8 * P], U8, tag="es", align_bytes=64)
             nc.vector.quantize_mx(
                 out=ec[:].bitcast(FP8X4),
                 scales=es[:],
-                in_=st[("gr", i)][:].rearrange("p g q t -> p (g q t)"),
+                in_=st[("gr", j)][:].rearrange("p k g q t -> p (k g q t)"),
             )
-            st[("ec", i)] = ec
-            st[("es", i)] = es
+            st[("ec", j)] = ec
+            st[("es", j)] = es
 
-        def mx_matmul(i):
-            hh = i // NPAL
-            j, k = divmod(i, 4)
-            if k == 0:
-                o_ps = ps_1.tile([P, 4, HD], FP32, tag="o_ps")
-                st[("o_ps", j)] = o_ps
-            ec, es = st[("ec", i)], st[("es", i)]
+        def mx_matmul(j):
+            hh = j // 2
+            o_ps = ps_1.tile([P, 4, HD], FP32, tag="o_ps")
+            st[("o_ps", j)] = o_ps
+            ec, es = st[("ec", j)], st[("es", j)]
             qc, qs = st[("qc", hh)], st[("qs", hh)]
-            for g in range(2):
-                cols = slice(g * P, (g + 1) * P)
-                nc.tensor.matmul_mx(
-                    out=st[("o_ps", j)][:, k, :],
-                    lhsT=ec[:, cols].bitcast(FP8X4),
-                    lhsT_scale=es[:, cols],
-                    rhs=qc[:, cols].bitcast(FP8X4),
-                    rhs_scale=qs[:, cols],
-                    start=(g == 0),
-                    stop=(g == 1),
-                )
+            for k in range(4):
+                for g in range(2):
+                    ecols = slice((2 * k + g) * P, (2 * k + g + 1) * P)
+                    qcols = slice(g * HD, (g + 1) * HD)
+                    nc.tensor.matmul_mx(
+                        out=o_ps[:, k, :],
+                        lhsT=ec[:, ecols].bitcast(FP8X4),
+                        lhsT_scale=es[:, ecols],
+                        rhs=qc[:, qcols].bitcast(FP8X4),
+                        rhs_scale=qs[:, qcols],
+                        start=(g == 0),
+                        stop=(g == 1),
+                    )
 
         def norm(j):
             hh, half = divmod(j, 2)
             b, h = divmod(hh, H)
-            rinv = small.tile([P, 4], FP32, tag="rinv")
+            rinv = deep.tile([P, 4], FP32, tag="rinv")
             nc.vector.reciprocal(out=rinv[:], in_=st[("rs", j)][:])
             o_sb = work.tile([P, 4, HD], FP32, tag="o_sb")
             nc.vector.tensor_tensor(out=o_sb[:], in0=st[("o_ps", j)][:],
@@ -196,36 +211,39 @@ def tile_palaceattention_kernel(tc, x, inter_palace_weight, out):
             prep_copy(0)
             prep_regroup(0)
             prep_quant(0)
-            for s in range(-2, NTILES + 4):
+            for s in range(-LEAD - 1, NTILES + 8):
                 hh, r = divmod(s, NPAL)
                 nxt = hh + 1
-                if ok(s + 2):
-                    qk(s + 2)
-                if ok(s + 1):
-                    pass_main(s + 1)
+                prep_ok = 0 <= s and nxt < NHEADS
                 if ok(s - 1):
                     transposes(s - 1)
-                if 0 <= s and nxt < NHEADS and r == 1:
+                if ok(s + LEAD + 1):
+                    qk(s + LEAD + 1)
+                if prep_ok and r == 1:
                     prep_transposes(nxt)
+                if ok(s + LEAD):
+                    pass_main(s + LEAD)
+                if ok(s + LEAD - 1):
+                    pass_fin(s + LEAD - 1)
                 if ok(s):
                     expo(s)
-                if ok(s - 2):
-                    quant(s - 2)
-                if ok(s + 1):
-                    pass_fin(s + 1)
                 if ok(s - 1):
                     evac(s - 1)
-                if 0 <= s and nxt < NHEADS:
-                    if r == 2:
-                        prep_copy(nxt)
-                    if r == 3:
-                        prep_regroup(nxt)
-                    if r == 4:
-                        prep_quant(nxt)
-                if ok(s - 3):
-                    mx_matmul(s - 3)
-                    if (s - 3) % 4 == 3:
-                        norm((s - 3) // 4)
+                if prep_ok and r == 2:
+                    prep_copy(nxt)
+                if ok(s - 2):
+                    regroup(s - 2)
+                if 0 <= s - 8 and hh < NHEADS and r == 0:
+                    prep_regroup(hh)
+                jq, rq = divmod(s - 5, 4)
+                if rq == 0 and 0 <= jq < NQUADS:
+                    if jq % 2 == 1 and jq // 2 + 1 < NHEADS:
+                        prep_quant(jq // 2 + 1)
+                    quant(jq)
+                jm, rm = divmod(s - 6, 4)
+                if rm == 0 and 0 <= jm < NQUADS:
+                    mx_matmul(jm)
+                    norm(jm)
 
         if PINNED:
             with tc.manual_schedule():

@@ -21,7 +21,7 @@ NQUADS = NTILES // 4
 SCALE = HD ** -0.5
 FLOPS = 2 * 2 * NB * H * T * T * HD
 PINNED = True
-DIRECT = (3,)
+DIRECT = (7,)
 LEAD = 2
 GR_BUFS = 1
 
@@ -46,17 +46,15 @@ def tile_palaceattention_kernel(tc, x, inter_palace_weight, out):
         x0 = const.tile([P, NPAL, H * HD], BF16)
         x1 = const.tile([P, NPAL, H * HD], BF16)
         xin = [x0, x1]
-        for b in range(NB):
-            for c in range(4):
-                cols = slice(c * 256, (c + 1) * 256)
-                nc.sync.dma_start(out=xin[b][:, :, cols], in_=xv[b][:, :, cols])
+        for b, c0, c1 in ((0, 0, 128), (0, 128, 256), (0, 256, 512), (0, 512, 1024), (1, 0, 512), (1, 512, 1024)):
+            nc.sync.dma_start(out=xin[b][:, :, c0:c1], in_=xv[b][:, :, c0:c1])
 
         ident = const.tile([P, P], BF16)
         make_identity(nc, ident[:])
         sig = const.tile([P, 1], FP32)
         nc.scalar.activation(out=sig[:], in_=w_bf[:], func=ACTF.Sigmoid)
-        csig = const.tile([P, 1], FP32)
-        nc.vector.tensor_scalar(out=csig[:], in0=sig[:], scalar1=SCALE, scalar2=None, op0=ALU.mult)
+        ncsig = const.tile([P, 1], FP32)
+        nc.vector.tensor_scalar(out=ncsig[:], in0=sig[:], scalar1=-SCALE, scalar2=None, op0=ALU.mult)
 
         st = {}
 
@@ -106,23 +104,26 @@ def tile_palaceattention_kernel(tc, x, inter_palace_weight, out):
                                      start=True, stop=True)
             st[("s", i)] = (s_a, s_b)
 
-        def pass_main(i):
-            s_a, s_b = st[("s", i)]
+        def pass_own(i):
+            s_a = st[("s", i)][0]
             sm = deep.tile([P, T], FP32, tag="sm")
-            mx = deep.tile([P, 4], FP32, tag="mx")
-            nc.vector.tensor_scalar(out=sm[:, 0:P], in0=s_a[:, 0:P], scalar1=SCALE, scalar2=None,
-                                    op0=ALU.mult, op1=ALU.max, accum_out=mx[:, 0:1])
-            nc.vector.tensor_scalar(out=sm[:, P:512], in0=s_a[:, P:512], scalar1=csig[:, 0:1], scalar2=None,
-                                    op0=ALU.mult, op1=ALU.max, accum_out=mx[:, 1:2])
-            nc.vector.tensor_scalar(out=sm[:, 512:T], in0=s_b[:], scalar1=csig[:, 0:1], scalar2=None,
-                                    op0=ALU.mult, op1=ALU.max, accum_out=mx[:, 2:3])
+            acc = deep.tile([P, 4], FP32, tag="acc")
+            nc.vector.tensor_scalar(out=sm[:, 0:P], in0=s_a[:, 0:P], scalar1=-SCALE, scalar2=None,
+                                    op0=ALU.mult, op1=ALU.min, accum_out=acc[:, 0:1])
             st[("sm", i)] = sm
-            st[("mx", i)] = mx
+            st[("acc", i)] = acc
 
-        def pass_fin(i):
-            nb = deep.tile([P, 1], FP32, tag="nb")
-            nc.vector.tensor_reduce(out=nb[:], in_=st[("mx", i)][:, 0:3], axis=AXIS.X, op=ALU.max, negate=True)
-            st[("nb", i)] = nb
+        def pass_a(i):
+            s_a = st[("s", i)][0]
+            acc = st[("acc", i)]
+            nc.vector.tensor_scalar(out=st[("sm", i)][:, P:512], in0=s_a[:, P:512], scalar1=ncsig[:, 0:1],
+                                    scalar2=acc[:, 0:1], op0=ALU.mult, op1=ALU.min, accum_out=acc[:, 1:2])
+
+        def pass_b(i):
+            s_b = st[("s", i)][1]
+            acc = st[("acc", i)]
+            nc.vector.tensor_scalar(out=st[("sm", i)][:, 512:T], in0=s_b[:], scalar1=ncsig[:, 0:1],
+                                    scalar2=acc[:, 1:2], op0=ALU.mult, op1=ALU.min, accum_out=acc[:, 2:3])
 
         def expo(i):
             j, k = divmod(i, 4)
@@ -130,8 +131,8 @@ def tile_palaceattention_kernel(tc, x, inter_palace_weight, out):
                 rs = deep.tile([P, 4], FP32, tag="rs")
                 st[("rs", j)] = rs
             e = work.tile([P, T], BF16, tag="e")
-            nc.scalar.activation(out=e[:], in_=st[("sm", i)][:], func=ACTF.Exp, bias=st[("nb", i)][:, 0:1],
-                                 scale=1.0, accum_out=st[("rs", j)][:, k:k + 1])
+            nc.scalar.activation(out=e[:], in_=st[("sm", i)][:], func=ACTF.Exp, bias=st[("acc", i)][:, 2:3],
+                                 scale=-1.0, accum_out=st[("rs", j)][:, k:k + 1])
             st[("e", i)] = e
 
         def transposes(i):
@@ -145,7 +146,7 @@ def tile_palaceattention_kernel(tc, x, inter_palace_weight, out):
         def evac(i):
             j, k = divmod(i, 4)
             xt = st[("xt", i)]
-            if k in DIRECT:
+            if i % NPAL in DIRECT:
                 nc.scalar.copy(out=st[("gr", j)][:, k], in_=xt[:].rearrange("p (g t) q -> p g q t", t=4))
             else:
                 tsb = deep.tile([P, NPAL, P], BF16, tag="tsb")
@@ -157,7 +158,7 @@ def tile_palaceattention_kernel(tc, x, inter_palace_weight, out):
             if k == 0:
                 gr = grp.tile([P, 4, 2, P, 4], BF16, tag="gr", align_bytes=64)
                 st[("gr", j)] = gr
-            if k not in DIRECT:
+            if i % NPAL not in DIRECT:
                 nc.gpsimd.tensor_scalar(out=st[("gr", j)][:, k],
                                         in0=st[("tsb", i)][:].rearrange("p (g t) q -> p g q t", t=4),
                                         scalar1=1.0, scalar2=0.0, op0=ALU.mult, op1=ALU.add)
@@ -211,7 +212,7 @@ def tile_palaceattention_kernel(tc, x, inter_palace_weight, out):
             prep_copy(0)
             prep_regroup(0)
             prep_quant(0)
-            for s in range(-LEAD - 1, NTILES + 8):
+            for s in range(-LEAD - 1, NTILES + 9):
                 hh, r = divmod(s, NPAL)
                 nxt = hh + 1
                 prep_ok = 0 <= s and nxt < NHEADS
@@ -221,26 +222,30 @@ def tile_palaceattention_kernel(tc, x, inter_palace_weight, out):
                     qk(s + LEAD + 1)
                 if prep_ok and r == 1:
                     prep_transposes(nxt)
+                if s + LEAD == -1:
+                    pass_own(0)
                 if ok(s + LEAD):
-                    pass_main(s + LEAD)
-                if ok(s + LEAD - 1):
-                    pass_fin(s + LEAD - 1)
+                    pass_a(s + LEAD)
+                if ok(s + LEAD) and ok(s + LEAD + 1):
+                    pass_own(s + LEAD + 1)
+                if ok(s + LEAD):
+                    pass_b(s + LEAD)
                 if ok(s):
                     expo(s)
                 if ok(s - 1):
                     evac(s - 1)
                 if prep_ok and r == 2:
                     prep_copy(nxt)
-                if ok(s - 2):
-                    regroup(s - 2)
-                if 0 <= s - 8 and hh < NHEADS and r == 0:
-                    prep_regroup(hh)
-                jq, rq = divmod(s - 5, 4)
+                jq, rq = divmod(s - 6, 4)
                 if rq == 0 and 0 <= jq < NQUADS:
                     if jq % 2 == 1 and jq // 2 + 1 < NHEADS:
                         prep_quant(jq // 2 + 1)
                     quant(jq)
-                jm, rm = divmod(s - 6, 4)
+                if ok(s - 2):
+                    regroup(s - 2)
+                if 0 <= s - 8 and hh < NHEADS and r == 0:
+                    prep_regroup(hh)
+                jm, rm = divmod(s - 7, 4)
                 if rm == 0 and 0 <= jm < NQUADS:
                     mx_matmul(jm)
                     norm(jm)

@@ -21,9 +21,19 @@ NQUADS = NTILES // 4
 SCALE = HD ** -0.5
 FLOPS = 2 * 2 * NB * H * T * T * HD
 PINNED = True
-DIRECT = (7,)
 LEAD = 2
-GR_BUFS = 1
+TAIL = NTILES - 4
+
+
+def route(i):
+    if i >= TAIL:
+        return "vector" if i % 2 == 0 else "scalar"
+    return "scalar" if i % NPAL == NPAL - 1 else "gpsimd"
+
+
+def tile_groups():
+    groups = [tuple(range(4 * j, 4 * j + 4)) for j in range(NQUADS - 1)]
+    return groups + [(TAIL, TAIL + 1), (TAIL + 2,), (TAIL + 3,)]
 
 
 def tile_palaceattention_kernel(tc, x, inter_palace_weight, out):
@@ -33,7 +43,7 @@ def tile_palaceattention_kernel(tc, x, inter_palace_weight, out):
         headp = ctx.enter_context(tc.tile_pool(name="headp", bufs=2))
         work = ctx.enter_context(tc.tile_pool(name="work", bufs=3))
         deep = ctx.enter_context(tc.tile_pool(name="deep", bufs=4))
-        grp = ctx.enter_context(tc.tile_pool(name="grp", bufs=GR_BUFS))
+        grp = ctx.enter_context(tc.tile_pool(name="grp", bufs=1))
         ps_s = ctx.enter_context(tc.psum_pool(name="ps_s", bufs=2))
         ps_x = ctx.enter_context(tc.psum_pool(name="ps_x", bufs=2))
         ps_1 = ctx.enter_context(tc.psum_pool(name="ps_1", bufs=1))
@@ -57,6 +67,16 @@ def tile_palaceattention_kernel(tc, x, inter_palace_weight, out):
         nc.vector.tensor_scalar(out=ncsig[:], in0=sig[:], scalar1=-SCALE, scalar2=None, op0=ALU.mult)
 
         st = {}
+        groups = tile_groups()
+        group_of = {}
+        quant_at = {}
+        mx_at = {}
+        for n, tiles in enumerate(groups):
+            for pos, i in enumerate(tiles):
+                group_of[i] = (n, pos)
+            slot = tiles[-1] + (2 if tiles[0] >= TAIL else 3)
+            quant_at[slot] = n
+            mx_at[slot + 1] = n
 
         def prep_transposes(hh):
             b, h = divmod(hh, H)
@@ -67,7 +87,11 @@ def tile_palaceattention_kernel(tc, x, inter_palace_weight, out):
 
         def prep_copy(hh):
             qt = headp.tile([P, NPAL * P], BF16, tag="qt")
-            nc.scalar.copy(out=qt[:], in_=st[("pt", hh)][:].rearrange("p a q -> p (a q)"))
+            src = st[("pt", hh)][:].rearrange("p a q -> p (a q)")
+            if hh % 2 == 1:
+                nc.vector.tensor_copy(out=qt[:], in_=src)
+            else:
+                nc.scalar.copy(out=qt[:], in_=src)
             st[("qt", hh)] = qt
 
         def prep_regroup(hh):
@@ -143,49 +167,60 @@ def tile_palaceattention_kernel(tc, x, inter_palace_weight, out):
                 nc.tensor.transpose(xt[:, (pq + k) % NPAL, :], e[:, k * P:(k + 1) * P], ident[:])
             st[("xt", i)] = xt
 
+        def grouped_tile(n):
+            if ("gr", n) not in st:
+                if groups[n][0] >= TAIL:
+                    grt = work.tile([P, len(groups[n]), 2, P, 4], BF16, tag="grt", align_bytes=64)
+                    st[("gr", n)] = grt
+                else:
+                    gr = grp.tile([P, 4, 2, P, 4], BF16, tag="gr", align_bytes=64)
+                    st[("gr", n)] = gr
+            return st[("gr", n)]
+
         def evac(i):
-            j, k = divmod(i, 4)
+            n, pos = group_of[i]
             xt = st[("xt", i)]
-            if i % NPAL in DIRECT:
-                nc.scalar.copy(out=st[("gr", j)][:, k], in_=xt[:].rearrange("p (g t) q -> p g q t", t=4))
-            else:
+            if route(i) == "gpsimd":
                 tsb = deep.tile([P, NPAL, P], BF16, tag="tsb")
                 nc.scalar.copy(out=tsb[:].rearrange("p a q -> p (a q)"), in_=xt[:].rearrange("p a q -> p (a q)"))
                 st[("tsb", i)] = tsb
+            elif route(i) == "scalar":
+                nc.scalar.copy(out=grouped_tile(n)[:, pos], in_=xt[:].rearrange("p (g t) q -> p g q t", t=4))
+            else:
+                nc.vector.tensor_copy(out=grouped_tile(n)[:, pos], in_=xt[:].rearrange("p (g t) q -> p g q t", t=4))
 
         def regroup(i):
-            j, k = divmod(i, 4)
-            if k == 0:
-                gr = grp.tile([P, 4, 2, P, 4], BF16, tag="gr", align_bytes=64)
-                st[("gr", j)] = gr
-            if i % NPAL not in DIRECT:
-                nc.gpsimd.tensor_scalar(out=st[("gr", j)][:, k],
+            n, pos = group_of[i]
+            if route(i) == "gpsimd":
+                nc.gpsimd.tensor_scalar(out=grouped_tile(n)[:, pos],
                                         in0=st[("tsb", i)][:].rearrange("p (g t) q -> p g q t", t=4),
                                         scalar1=1.0, scalar2=0.0, op0=ALU.mult, op1=ALU.add)
 
-        def quant(j):
-            ec = headp.tile([P, 8 * P], U32, tag="ec", align_bytes=64)
-            es = headp.tile([P, 8 * P], U8, tag="es", align_bytes=64)
+        def quant(n):
+            width = 2 * P * len(groups[n])
+            ec = headp.tile([P, width], U32, tag="ec", align_bytes=64)
+            es = headp.tile([P, width], U8, tag="es", align_bytes=64)
             nc.vector.quantize_mx(
                 out=ec[:].bitcast(FP8X4),
                 scales=es[:],
-                in_=st[("gr", j)][:].rearrange("p k g q t -> p (k g q t)"),
+                in_=st[("gr", n)][:].rearrange("p k g q t -> p (k g q t)"),
             )
-            st[("ec", j)] = ec
-            st[("es", j)] = es
+            st[("ec", n)] = ec
+            st[("es", n)] = es
 
-        def mx_matmul(j):
-            hh = j // 2
-            o_ps = ps_1.tile([P, 4, HD], FP32, tag="o_ps")
-            st[("o_ps", j)] = o_ps
-            ec, es = st[("ec", j)], st[("es", j)]
-            qc, qs = st[("qc", hh)], st[("qs", hh)]
-            for k in range(4):
+        def mx_matmul(n):
+            ec, es = st[("ec", n)], st[("es", n)]
+            for pos, i in enumerate(groups[n]):
+                j, k = divmod(i, 4)
+                if k == 0:
+                    o_ps = ps_1.tile([P, 4, HD], FP32, tag="o_ps")
+                    st[("o_ps", j)] = o_ps
+                qc, qs = st[("qc", i // NPAL)], st[("qs", i // NPAL)]
                 for g in range(2):
-                    ecols = slice((2 * k + g) * P, (2 * k + g + 1) * P)
+                    ecols = slice((2 * pos + g) * P, (2 * pos + g + 1) * P)
                     qcols = slice(g * HD, (g + 1) * HD)
                     nc.tensor.matmul_mx(
-                        out=o_ps[:, k, :],
+                        out=st[("o_ps", j)][:, k, :],
                         lhsT=ec[:, ecols].bitcast(FP8X4),
                         lhsT_scale=es[:, ecols],
                         rhs=qc[:, qcols].bitcast(FP8X4),
@@ -193,6 +228,8 @@ def tile_palaceattention_kernel(tc, x, inter_palace_weight, out):
                         start=(g == 0),
                         stop=(g == 1),
                     )
+                if k == 3:
+                    norm(j)
 
         def norm(j):
             hh, half = divmod(j, 2)
@@ -236,19 +273,17 @@ def tile_palaceattention_kernel(tc, x, inter_palace_weight, out):
                     evac(s - 1)
                 if prep_ok and r == 2:
                     prep_copy(nxt)
-                jq, rq = divmod(s - 6, 4)
-                if rq == 0 and 0 <= jq < NQUADS:
-                    if jq % 2 == 1 and jq // 2 + 1 < NHEADS:
-                        prep_quant(jq // 2 + 1)
-                    quant(jq)
+                if s in quant_at:
+                    following = groups[quant_at[s]][-1] + 1
+                    if following % NPAL == 0 and following < NTILES:
+                        prep_quant(following // NPAL)
+                    quant(quant_at[s])
                 if ok(s - 2):
                     regroup(s - 2)
                 if 0 <= s - 8 and hh < NHEADS and r == 0:
                     prep_regroup(hh)
-                jm, rm = divmod(s - 7, 4)
-                if rm == 0 and 0 <= jm < NQUADS:
-                    mx_matmul(jm)
-                    norm(jm)
+                if s in mx_at:
+                    mx_matmul(mx_at[s])
 
         if PINNED:
             with tc.manual_schedule():

@@ -87,11 +87,7 @@ def tile_palaceattention_kernel(tc, x, inter_palace_weight, out):
 
         def prep_copy(hh):
             qt = headp.tile([P, NPAL * P], BF16, tag="qt")
-            src = st[("pt", hh)][:].rearrange("p a q -> p (a q)")
-            if hh % 2 == 1:
-                nc.vector.tensor_copy(out=qt[:], in_=src)
-            else:
-                nc.scalar.copy(out=qt[:], in_=src)
+            nc.scalar.copy(out=qt[:], in_=st[("pt", hh)][:].rearrange("p a q -> p (a q)"))
             st[("qt", hh)] = qt
 
         def prep_regroup(hh):
@@ -247,6 +243,8 @@ def tile_palaceattention_kernel(tc, x, inter_palace_weight, out):
         def body():
             prep_transposes(0)
             prep_copy(0)
+            warm = const.tile([P, 1], FP32)
+            nc.scalar.activation(out=warm[:], in_=sig[:], func=ACTF.Exp)
             prep_regroup(0)
             prep_quant(0)
             for s in range(-LEAD - 1, NTILES + 9):

@@ -10,19 +10,23 @@ U8 = mybir.dt.uint8
 FP8X4 = mybir.dt.float8_e4m3fn_x4
 ALU = mybir.AluOpType
 ACTF = mybir.ActivationFunctionType
-AXIS = mybir.AxisListType
 
 NB, T, H, HD = 2, 1024, 8, 128
 NPAL = 8
 P = 128
+PACK = 4
+PASSES = T // (P * PACK)
+BANK = 512
+BANK_PALACES = BANK // P
 NHEADS = NB * H
 NTILES = NHEADS * NPAL
-NQUADS = NTILES // 4
+QUAD = 4
 SCALE = HD ** -0.5
 FLOPS = 2 * 2 * NB * H * T * T * HD
-PINNED = True
+
 LEAD = 2
-TAIL = NTILES - 4
+TAIL = NTILES - QUAD
+LOADS = ((0, 0, 128), (0, 128, 256), (0, 256, 512), (0, 512, 1024), (1, 0, 512), (1, 512, 1024))
 
 
 def route(i):
@@ -31,8 +35,13 @@ def route(i):
     return "scalar" if i % NPAL == NPAL - 1 else "gpsimd"
 
 
+def partner(i):
+    other = i + 1 if i % 2 == 0 else i - 1
+    return other if route(i) == "gpsimd" and route(other) == "gpsimd" else None
+
+
 def tile_groups():
-    groups = [tuple(range(4 * j, 4 * j + 4)) for j in range(NQUADS - 1)]
+    groups = [tuple(range(QUAD * j, QUAD * j + QUAD)) for j in range(NTILES // QUAD - 1)]
     return groups + [(TAIL, TAIL + 1), (TAIL + 2,), (TAIL + 3,)]
 
 
@@ -48,15 +57,15 @@ def tile_palaceattention_kernel(tc, x, inter_palace_weight, out):
         ps_x = ctx.enter_context(tc.psum_pool(name="ps_x", bufs=2))
         ps_1 = ctx.enter_context(tc.psum_pool(name="ps_1", bufs=1))
 
-        xv = [x[b].rearrange("(a p) c -> a p c", p=NPAL) for b in range(NB)]
-        ov = [out[b].rearrange("(a p) c -> a p c", p=NPAL) for b in range(NB)]
+        xv = [x[b].rearrange("(a l) c -> a l c", l=NPAL) for b in range(NB)]
+        ov = [out[b].rearrange("(a l) c -> a l c", l=NPAL) for b in range(NB)]
 
         w_bf = const.tile([P, 1], BF16)
         nc.sync.dma_start(out=w_bf[:], in_=inter_palace_weight.partition_broadcast(P))
         x0 = const.tile([P, NPAL, H * HD], BF16)
         x1 = const.tile([P, NPAL, H * HD], BF16)
         xin = [x0, x1]
-        for b, c0, c1 in ((0, 0, 128), (0, 128, 256), (0, 256, 512), (0, 512, 1024), (1, 0, 512), (1, 512, 1024)):
+        for b, c0, c1 in LOADS:
             nc.sync.dma_start(out=xin[b][:, :, c0:c1], in_=xv[b][:, :, c0:c1])
 
         ident = const.tile([P, P], BF16)
@@ -74,32 +83,32 @@ def tile_palaceattention_kernel(tc, x, inter_palace_weight, out):
         for n, tiles in enumerate(groups):
             for pos, i in enumerate(tiles):
                 group_of[i] = (n, pos)
-            slot = tiles[-1] + (2 if tiles[0] >= TAIL else 3)
-            quant_at[slot] = n
-            mx_at[slot + 1] = n
+            step = tiles[-1] + (2 if tiles[0] >= TAIL else 3)
+            quant_at[step] = n
+            mx_at[step + 1] = n
 
-        def prep_transposes(hh):
+        def q_transposes(hh):
             b, h = divmod(hh, H)
             pt = ps_1.tile([P, NPAL, P], BF16, tag="pt")
             for pal in range(NPAL):
                 nc.tensor.transpose(pt[:, pal, :], xin[b][:, pal, h * HD:(h + 1) * HD], ident[:])
             st[("pt", hh)] = pt
 
-        def prep_copy(hh):
+        def q_copy(hh):
             qt = headp.tile([P, NPAL * P], BF16, tag="qt")
-            nc.scalar.copy(out=qt[:], in_=st[("pt", hh)][:].rearrange("p a q -> p (a q)"))
+            nc.scalar.copy(out=qt[:], in_=st[("pt", hh)][:].rearrange("p l y -> p (l y)"))
             st[("qt", hh)] = qt
 
-        def prep_regroup(hh):
+        def q_regroup(hh):
             b, h = divmod(hh, H)
-            qg = headp.tile([P, 2, HD, 4], BF16, tag="qg", align_bytes=64)
-            src = xin[b][:, :, h * HD:(h + 1) * HD].rearrange("p (g t) d -> p g d t", t=4)
+            qg = headp.tile([P, PASSES, HD, PACK], BF16, tag="qg", align_bytes=64)
+            src = xin[b][:, :, h * HD:(h + 1) * HD].rearrange("p (g t) d -> p g d t", t=PACK)
             nc.gpsimd.tensor_scalar(out=qg[:], in0=src, scalar1=1.0, scalar2=0.0, op0=ALU.mult, op1=ALU.add)
             st[("qg", hh)] = qg
 
-        def prep_quant(hh):
-            qc = headp.tile([P, 2 * HD], U32, tag="qc", align_bytes=64)
-            qs = headp.tile([P, 2 * HD], U8, tag="qs", align_bytes=64)
+        def q_quantise(hh):
+            qc = headp.tile([P, PASSES * HD], U32, tag="qc", align_bytes=64)
+            qs = headp.tile([P, PASSES * HD], U8, tag="qs", align_bytes=64)
             nc.vector.quantize_mx(
                 out=qc[:].bitcast(FP8X4),
                 scales=qs[:],
@@ -108,23 +117,23 @@ def tile_palaceattention_kernel(tc, x, inter_palace_weight, out):
             st[("qc", hh)] = qc
             st[("qs", hh)] = qs
 
-        def qk(i):
-            hh, pq = divmod(i, NPAL)
+        def scores(i):
+            hh, own = divmod(i, NPAL)
             qt = st[("qt", hh)]
-            lhs = qt[:, pq * P:(pq + 1) * P]
-            s_a = ps_s.tile([P, 512], FP32, tag="s_a")
-            s_b = ps_s.tile([P, 512], FP32, tag="s_b")
+            lhs = qt[:, own * P:(own + 1) * P]
+            s_a = ps_s.tile([P, BANK], FP32, tag="s_a")
+            s_b = ps_s.tile([P, BANK], FP32, tag="s_b")
             for bank, dst in ((0, s_a), (1, s_b)):
-                first = (pq + 4 * bank) % NPAL
-                n1 = min(4, NPAL - first)
+                first = (own + BANK_PALACES * bank) % NPAL
+                n1 = min(BANK_PALACES, NPAL - first)
                 nc.tensor.matmul(dst[:, 0:n1 * P], lhsT=lhs, rhs=qt[:, first * P:(first + n1) * P],
                                  start=True, stop=True)
-                if n1 < 4:
-                    nc.tensor.matmul(dst[:, n1 * P:512], lhsT=lhs, rhs=qt[:, 0:(4 - n1) * P],
+                if n1 < BANK_PALACES:
+                    nc.tensor.matmul(dst[:, n1 * P:BANK], lhsT=lhs, rhs=qt[:, 0:(BANK_PALACES - n1) * P],
                                      start=True, stop=True)
             st[("s", i)] = (s_a, s_b)
 
-        def pass_own(i):
+        def scale_own(i):
             s_a = st[("s", i)][0]
             sm = deep.tile([P, T], FP32, tag="sm")
             acc = deep.tile([P, 4], FP32, tag="acc")
@@ -133,87 +142,93 @@ def tile_palaceattention_kernel(tc, x, inter_palace_weight, out):
             st[("sm", i)] = sm
             st[("acc", i)] = acc
 
-        def pass_a(i):
+        def scale_rest_of_bank(i):
             s_a = st[("s", i)][0]
             acc = st[("acc", i)]
-            nc.vector.tensor_scalar(out=st[("sm", i)][:, P:512], in0=s_a[:, P:512], scalar1=ncsig[:, 0:1],
+            nc.vector.tensor_scalar(out=st[("sm", i)][:, P:BANK], in0=s_a[:, P:BANK], scalar1=ncsig[:, 0:1],
                                     scalar2=acc[:, 0:1], op0=ALU.mult, op1=ALU.min, accum_out=acc[:, 1:2])
 
-        def pass_b(i):
+        def scale_second_bank(i):
             s_b = st[("s", i)][1]
             acc = st[("acc", i)]
-            nc.vector.tensor_scalar(out=st[("sm", i)][:, 512:T], in0=s_b[:], scalar1=ncsig[:, 0:1],
+            nc.vector.tensor_scalar(out=st[("sm", i)][:, BANK:T], in0=s_b[:], scalar1=ncsig[:, 0:1],
                                     scalar2=acc[:, 1:2], op0=ALU.mult, op1=ALU.min, accum_out=acc[:, 2:3])
 
-        def expo(i):
-            j, k = divmod(i, 4)
+        def exponential(i):
+            j, k = divmod(i, QUAD)
             if k == 0:
-                rs = deep.tile([P, 4], FP32, tag="rs")
+                rs = deep.tile([P, QUAD], FP32, tag="rs")
                 st[("rs", j)] = rs
             e = work.tile([P, T], BF16, tag="e")
             nc.scalar.activation(out=e[:], in_=st[("sm", i)][:], func=ACTF.Exp, bias=st[("acc", i)][:, 2:3],
                                  scale=-1.0, accum_out=st[("rs", j)][:, k:k + 1])
             st[("e", i)] = e
 
-        def transposes(i):
-            pq = i % NPAL
+        def e_transposes(i):
+            own = i % NPAL
             e = st[("e", i)]
             xt = ps_x.tile([P, NPAL, P], BF16, tag="xt")
-            for k in range(NPAL):
-                nc.tensor.transpose(xt[:, (pq + k) % NPAL, :], e[:, k * P:(k + 1) * P], ident[:])
+            for blk in range(NPAL):
+                nc.tensor.transpose(xt[:, (own + blk) % NPAL, :], e[:, blk * P:(blk + 1) * P], ident[:])
             st[("xt", i)] = xt
 
         def grouped_tile(n):
             if ("gr", n) not in st:
                 if groups[n][0] >= TAIL:
-                    grt = work.tile([P, len(groups[n]), 2, P, 4], BF16, tag="grt", align_bytes=64)
+                    grt = work.tile([P, len(groups[n]), PASSES, P, PACK], BF16, tag="grt", align_bytes=64)
                     st[("gr", n)] = grt
                 else:
-                    gr = grp.tile([P, 4, 2, P, 4], BF16, tag="gr", align_bytes=64)
+                    gr = grp.tile([P, QUAD, PASSES, P, PACK], BF16, tag="gr", align_bytes=64)
                     st[("gr", n)] = gr
             return st[("gr", n)]
 
-        def evac(i):
+        def copy_out(i):
             n, pos = group_of[i]
             xt = st[("xt", i)]
             if route(i) == "gpsimd":
-                tsb = deep.tile([P, NPAL, P], BF16, tag="tsb")
-                nc.scalar.copy(out=tsb[:].rearrange("p a q -> p (a q)"), in_=xt[:].rearrange("p a q -> p (a q)"))
-                st[("tsb", i)] = tsb
+                if partner(i) is None or i % 2 == 0:
+                    tsb = deep.tile([P, 2, NPAL, P], BF16, tag="tsb")
+                    st[("tsb", i // 2)] = tsb
+                nc.scalar.copy(out=st[("tsb", i // 2)][:, i % 2].rearrange("p l y -> p (l y)"),
+                               in_=xt[:].rearrange("p l y -> p (l y)"))
             elif route(i) == "scalar":
-                nc.scalar.copy(out=grouped_tile(n)[:, pos], in_=xt[:].rearrange("p (g t) q -> p g q t", t=4))
+                nc.scalar.copy(out=grouped_tile(n)[:, pos], in_=xt[:].rearrange("p (g t) y -> p g y t", t=PACK))
             else:
-                nc.vector.tensor_copy(out=grouped_tile(n)[:, pos], in_=xt[:].rearrange("p (g t) q -> p g q t", t=4))
+                nc.vector.tensor_copy(out=grouped_tile(n)[:, pos], in_=xt[:].rearrange("p (g t) y -> p g y t", t=PACK))
 
         def regroup(i):
             n, pos = group_of[i]
-            if route(i) == "gpsimd":
+            if route(i) == "gpsimd" and partner(i) is None:
                 nc.gpsimd.tensor_scalar(out=grouped_tile(n)[:, pos],
-                                        in0=st[("tsb", i)][:].rearrange("p (g t) q -> p g q t", t=4),
+                                        in0=st[("tsb", i // 2)][:, i % 2].rearrange("p (g t) y -> p g y t", t=PACK),
+                                        scalar1=1.0, scalar2=0.0, op0=ALU.mult, op1=ALU.add)
+            elif route(i) == "gpsimd" and i % 2 == 1:
+                nc.gpsimd.tensor_scalar(out=grouped_tile(n)[:, pos - 1:pos + 1].rearrange("p i g y t -> p (i g) y t"),
+                                        in0=st[("tsb", i // 2)][:].rearrange("p i (g t) y -> p (i g) y t", t=PACK),
                                         scalar1=1.0, scalar2=0.0, op0=ALU.mult, op1=ALU.add)
 
-        def quant(n):
-            width = 2 * P * len(groups[n])
+        def quantise(n):
+            width = PASSES * P * len(groups[n])
             ec = headp.tile([P, width], U32, tag="ec", align_bytes=64)
             es = headp.tile([P, width], U8, tag="es", align_bytes=64)
             nc.vector.quantize_mx(
                 out=ec[:].bitcast(FP8X4),
                 scales=es[:],
-                in_=st[("gr", n)][:].rearrange("p k g q t -> p (k g q t)"),
+                in_=st[("gr", n)][:].rearrange("p i g y t -> p (i g y t)"),
             )
             st[("ec", n)] = ec
             st[("es", n)] = es
 
-        def mx_matmul(n):
+        def multiply(n):
             ec, es = st[("ec", n)], st[("es", n)]
             for pos, i in enumerate(groups[n]):
-                j, k = divmod(i, 4)
+                j, k = divmod(i, QUAD)
                 if k == 0:
-                    o_ps = ps_1.tile([P, 4, HD], FP32, tag="o_ps")
+                    o_ps = ps_1.tile([P, QUAD, HD], FP32, tag="o_ps")
                     st[("o_ps", j)] = o_ps
                 qc, qs = st[("qc", i // NPAL)], st[("qs", i // NPAL)]
-                for g in range(2):
-                    ecols = slice((2 * pos + g) * P, (2 * pos + g + 1) * P)
+                for g in range(PASSES):
+                    ecols = slice((PASSES * pos + g) * P, (PASSES * pos + g + 1) * P)
                     qcols = slice(g * HD, (g + 1) * HD)
                     nc.tensor.matmul_mx(
                         out=st[("o_ps", j)][:, k, :],
@@ -222,69 +237,63 @@ def tile_palaceattention_kernel(tc, x, inter_palace_weight, out):
                         rhs=qc[:, qcols].bitcast(FP8X4),
                         rhs_scale=qs[:, qcols],
                         start=(g == 0),
-                        stop=(g == 1),
+                        stop=(g == PASSES - 1),
                     )
-                if k == 3:
-                    norm(j)
+                if k == QUAD - 1:
+                    divide_and_store(j)
 
-        def norm(j):
-            hh, half = divmod(j, 2)
+        def divide_and_store(j):
+            hh, half = divmod(j, NPAL // QUAD)
             b, h = divmod(hh, H)
-            rinv = deep.tile([P, 4], FP32, tag="rinv")
+            rinv = deep.tile([P, QUAD], FP32, tag="rinv")
             nc.vector.reciprocal(out=rinv[:], in_=st[("rs", j)][:])
-            o_sb = work.tile([P, 4, HD], FP32, tag="o_sb")
+            o_sb = work.tile([P, QUAD, HD], FP32, tag="o_sb")
             nc.vector.tensor_tensor(out=o_sb[:], in0=st[("o_ps", j)][:],
-                                    in1=rinv[:].unsqueeze(2).to_broadcast([P, 4, HD]), op=ALU.mult)
-            nc.sync.dma_start(out=ov[b][:, half * 4:(half + 1) * 4, h * HD:(h + 1) * HD], in_=o_sb[:])
+                                    in1=rinv[:].unsqueeze(2).to_broadcast([P, QUAD, HD]), op=ALU.mult)
+            nc.sync.dma_start(out=ov[b][:, half * QUAD:(half + 1) * QUAD, h * HD:(h + 1) * HD], in_=o_sb[:])
 
-        def ok(i):
+        def is_tile(i):
             return 0 <= i < NTILES
 
-        def body():
-            prep_transposes(0)
-            prep_copy(0)
+        with tc.manual_schedule():
+            q_transposes(0)
+            q_copy(0)
             warm = const.tile([P, 1], FP32)
             nc.scalar.activation(out=warm[:], in_=sig[:], func=ACTF.Exp)
-            prep_regroup(0)
-            prep_quant(0)
-            for s in range(-LEAD - 1, NTILES + 9):
+            q_regroup(0)
+            q_quantise(0)
+            for s in range(-LEAD - 1, max(mx_at) + 1):
                 hh, r = divmod(s, NPAL)
-                nxt = hh + 1
-                prep_ok = 0 <= s and nxt < NHEADS
-                if ok(s - 1):
-                    transposes(s - 1)
-                if ok(s + LEAD + 1):
-                    qk(s + LEAD + 1)
-                if prep_ok and r == 1:
-                    prep_transposes(nxt)
+                following_head = hh + 1
+                head_follows = 0 <= s and following_head < NHEADS
+                if is_tile(s - 1):
+                    e_transposes(s - 1)
+                if is_tile(s + LEAD + 1):
+                    scores(s + LEAD + 1)
+                if head_follows and r == 1:
+                    q_transposes(following_head)
                 if s + LEAD == -1:
-                    pass_own(0)
-                if ok(s + LEAD):
-                    pass_a(s + LEAD)
-                if ok(s + LEAD) and ok(s + LEAD + 1):
-                    pass_own(s + LEAD + 1)
-                if ok(s + LEAD):
-                    pass_b(s + LEAD)
-                if ok(s):
-                    expo(s)
-                if ok(s - 1):
-                    evac(s - 1)
-                if prep_ok and r == 2:
-                    prep_copy(nxt)
+                    scale_own(0)
+                if is_tile(s + LEAD):
+                    scale_rest_of_bank(s + LEAD)
+                if is_tile(s + LEAD) and is_tile(s + LEAD + 1):
+                    scale_own(s + LEAD + 1)
+                if is_tile(s + LEAD):
+                    scale_second_bank(s + LEAD)
+                if is_tile(s):
+                    exponential(s)
+                if is_tile(s - 1):
+                    copy_out(s - 1)
+                if head_follows and r == 2:
+                    q_copy(following_head)
                 if s in quant_at:
-                    following = groups[quant_at[s]][-1] + 1
-                    if following % NPAL == 0 and following < NTILES:
-                        prep_quant(following // NPAL)
-                    quant(quant_at[s])
-                if ok(s - 2):
+                    next_tile = groups[quant_at[s]][-1] + 1
+                    if next_tile % NPAL == 0 and next_tile < NTILES:
+                        q_quantise(next_tile // NPAL)
+                    quantise(quant_at[s])
+                if is_tile(s - 2):
                     regroup(s - 2)
-                if 0 <= s - 8 and hh < NHEADS and r == 0:
-                    prep_regroup(hh)
+                if 0 <= s - NPAL and hh < NHEADS and r == 0:
+                    q_regroup(hh)
                 if s in mx_at:
-                    mx_matmul(mx_at[s])
-
-        if PINNED:
-            with tc.manual_schedule():
-                body()
-        else:
-            body()
+                    multiply(mx_at[s])

@@ -29,15 +29,8 @@ TAIL = NTILES - QUAD
 LOADS = ((0, 0, 128), (0, 128, 256), (0, 256, 512), (0, 512, 1024), (1, 0, 512), (1, 512, 1024))
 
 
-def route(i):
-    if i >= TAIL:
-        return "vector" if i % 2 == 0 else "scalar"
-    return "scalar" if i % NPAL == NPAL - 1 else "gpsimd"
-
-
-def partner(i):
-    other = i + 1 if i % 2 == 0 else i - 1
-    return other if route(i) == "gpsimd" and route(other) == "gpsimd" else None
+def first_palace(own):
+    return own if own % 2 == 0 else (own - BANK_PALACES + 1) % NPAL
 
 
 def tile_groups():
@@ -52,7 +45,7 @@ def tile_palaceattention_kernel(tc, x, inter_palace_weight, out):
         headp = ctx.enter_context(tc.tile_pool(name="headp", bufs=2))
         work = ctx.enter_context(tc.tile_pool(name="work", bufs=3))
         deep = ctx.enter_context(tc.tile_pool(name="deep", bufs=4))
-        grp = ctx.enter_context(tc.tile_pool(name="grp", bufs=1))
+        grp = ctx.enter_context(tc.tile_pool(name="grp", bufs=2))
         ps_s = ctx.enter_context(tc.psum_pool(name="ps_s", bufs=2))
         ps_x = ctx.enter_context(tc.psum_pool(name="ps_x", bufs=2))
         ps_1 = ctx.enter_context(tc.psum_pool(name="ps_1", bufs=1))
@@ -70,6 +63,8 @@ def tile_palaceattention_kernel(tc, x, inter_palace_weight, out):
 
         ident = const.tile([P, P], BF16)
         make_identity(nc, ident[:])
+        ident_f32 = const.tile([P, P], FP32)
+        make_identity(nc, ident_f32[:])
         sig = const.tile([P, 1], FP32)
         nc.scalar.activation(out=sig[:], in_=w_bf[:], func=ACTF.Sigmoid)
         ncsig = const.tile([P, 1], FP32)
@@ -83,7 +78,7 @@ def tile_palaceattention_kernel(tc, x, inter_palace_weight, out):
         for n, tiles in enumerate(groups):
             for pos, i in enumerate(tiles):
                 group_of[i] = (n, pos)
-            step = tiles[-1] + (2 if tiles[0] >= TAIL else 3)
+            step = tiles[-1] + 2
             quant_at[step] = n
             mx_at[step + 1] = n
 
@@ -124,7 +119,7 @@ def tile_palaceattention_kernel(tc, x, inter_palace_weight, out):
             s_a = ps_s.tile([P, BANK], FP32, tag="s_a")
             s_b = ps_s.tile([P, BANK], FP32, tag="s_b")
             for bank, dst in ((0, s_a), (1, s_b)):
-                first = (own + BANK_PALACES * bank) % NPAL
+                first = (first_palace(own) + BANK_PALACES * bank) % NPAL
                 n1 = min(BANK_PALACES, NPAL - first)
                 nc.tensor.matmul(dst[:, 0:n1 * P], lhsT=lhs, rhs=qt[:, first * P:(first + n1) * P],
                                  start=True, stop=True)
@@ -133,11 +128,15 @@ def tile_palaceattention_kernel(tc, x, inter_palace_weight, out):
                                      start=True, stop=True)
             st[("s", i)] = (s_a, s_b)
 
+        def own_columns(i):
+            return slice(0, P) if i % 2 == 0 else slice(BANK - P, BANK)
+
         def scale_own(i):
             s_a = st[("s", i)][0]
             sm = deep.tile([P, T], FP32, tag="sm")
             acc = deep.tile([P, 4], FP32, tag="acc")
-            nc.vector.tensor_scalar(out=sm[:, 0:P], in0=s_a[:, 0:P], scalar1=-SCALE, scalar2=None,
+            cols = own_columns(i)
+            nc.vector.tensor_scalar(out=sm[:, cols], in0=s_a[:, cols], scalar1=-SCALE, scalar2=None,
                                     op0=ALU.mult, op1=ALU.min, accum_out=acc[:, 0:1])
             st[("sm", i)] = sm
             st[("acc", i)] = acc
@@ -145,7 +144,8 @@ def tile_palaceattention_kernel(tc, x, inter_palace_weight, out):
         def scale_rest_of_bank(i):
             s_a = st[("s", i)][0]
             acc = st[("acc", i)]
-            nc.vector.tensor_scalar(out=st[("sm", i)][:, P:BANK], in0=s_a[:, P:BANK], scalar1=ncsig[:, 0:1],
+            cols = slice(P, BANK) if i % 2 == 0 else slice(0, BANK - P)
+            nc.vector.tensor_scalar(out=st[("sm", i)][:, cols], in0=s_a[:, cols], scalar1=ncsig[:, 0:1],
                                     scalar2=acc[:, 0:1], op0=ALU.mult, op1=ALU.min, accum_out=acc[:, 1:2])
 
         def scale_second_bank(i):
@@ -160,52 +160,33 @@ def tile_palaceattention_kernel(tc, x, inter_palace_weight, out):
                 rs = deep.tile([P, QUAD], FP32, tag="rs")
                 st[("rs", j)] = rs
             e = work.tile([P, T], BF16, tag="e")
-            nc.scalar.activation(out=e[:], in_=st[("sm", i)][:], func=ACTF.Exp, bias=st[("acc", i)][:, 2:3],
+            nc.scalar.activation(out=e[:].rearrange("p (u a e) -> p u a e", a=P, e=2),
+                                 in_=st[("sm", i)][:].rearrange("p (u e a) -> p u a e", a=P, e=2), func=ACTF.Exp, bias=st[("acc", i)][:, 2:3],
                                  scale=-1.0, accum_out=st[("rs", j)][:, k:k + 1])
             st[("e", i)] = e
 
         def e_transposes(i):
-            own = i % NPAL
-            e = st[("e", i)]
-            xt = ps_x.tile([P, NPAL, P], BF16, tag="xt")
-            for blk in range(NPAL):
-                nc.tensor.transpose(xt[:, (own + blk) % NPAL, :], e[:, blk * P:(blk + 1) * P], ident[:])
+            first = first_palace(i % NPAL) // 2
+            words = st[("e", i)][:].bitcast(FP32)
+            xt = ps_x.tile([P, NPAL // 2, P], FP32, tag="xt")
+            for u in range(NPAL // 2):
+                nc.tensor.transpose(xt[:, (first + u) % (NPAL // 2), :], words[:, u * P:(u + 1) * P], ident_f32[:])
             st[("xt", i)] = xt
 
         def grouped_tile(n):
             if ("gr", n) not in st:
-                if groups[n][0] >= TAIL:
-                    grt = work.tile([P, len(groups[n]), PASSES, P, PACK], BF16, tag="grt", align_bytes=64)
-                    st[("gr", n)] = grt
-                else:
-                    gr = grp.tile([P, QUAD, PASSES, P, PACK], BF16, tag="gr", align_bytes=64)
-                    st[("gr", n)] = gr
+                gr = grp.tile([P, len(groups[n]), PASSES * P * PACK], BF16, tag="gr%d" % len(groups[n]), align_bytes=64)
+                st[("gr", n)] = gr
             return st[("gr", n)]
 
         def copy_out(i):
             n, pos = group_of[i]
-            xt = st[("xt", i)]
-            if route(i) == "gpsimd":
-                if partner(i) is None or i % 2 == 0:
-                    tsb = deep.tile([P, 2, NPAL, P], BF16, tag="tsb")
-                    st[("tsb", i // 2)] = tsb
-                nc.scalar.copy(out=st[("tsb", i // 2)][:, i % 2].rearrange("p l y -> p (l y)"),
-                               in_=xt[:].rearrange("p l y -> p (l y)"))
-            elif route(i) == "scalar":
-                nc.scalar.copy(out=grouped_tile(n)[:, pos], in_=xt[:].rearrange("p (g t) y -> p g y t", t=PACK))
+            dst = grouped_tile(n)[:, pos, :].bitcast(FP32).rearrange("p (g y u) -> p g y u", g=PASSES, u=2)
+            src = st[("xt", i)][:].rearrange("p (g u) y -> p g y u", u=2)
+            if i >= TAIL and i % 2 == 0:
+                nc.vector.tensor_copy(out=dst, in_=src)
             else:
-                nc.vector.tensor_copy(out=grouped_tile(n)[:, pos], in_=xt[:].rearrange("p (g t) y -> p g y t", t=PACK))
-
-        def regroup(i):
-            n, pos = group_of[i]
-            if route(i) == "gpsimd" and partner(i) is None:
-                nc.gpsimd.tensor_scalar(out=grouped_tile(n)[:, pos],
-                                        in0=st[("tsb", i // 2)][:, i % 2].rearrange("p (g t) y -> p g y t", t=PACK),
-                                        scalar1=1.0, scalar2=0.0, op0=ALU.mult, op1=ALU.add)
-            elif route(i) == "gpsimd" and i % 2 == 1:
-                nc.gpsimd.tensor_scalar(out=grouped_tile(n)[:, pos - 1:pos + 1].rearrange("p i g y t -> p (i g) y t"),
-                                        in0=st[("tsb", i // 2)][:].rearrange("p i (g t) y -> p (i g) y t", t=PACK),
-                                        scalar1=1.0, scalar2=0.0, op0=ALU.mult, op1=ALU.add)
+                nc.scalar.copy(out=dst, in_=src)
 
         def quantise(n):
             width = PASSES * P * len(groups[n])
@@ -214,7 +195,7 @@ def tile_palaceattention_kernel(tc, x, inter_palace_weight, out):
             nc.vector.quantize_mx(
                 out=ec[:].bitcast(FP8X4),
                 scales=es[:],
-                in_=st[("gr", n)][:].rearrange("p i g y t -> p (i g y t)"),
+                in_=st[("gr", n)][:].rearrange("p i k -> p (i k)"),
             )
             st[("ec", n)] = ec
             st[("es", n)] = es
@@ -291,8 +272,6 @@ def tile_palaceattention_kernel(tc, x, inter_palace_weight, out):
                     if next_tile % NPAL == 0 and next_tile < NTILES:
                         q_quantise(next_tile // NPAL)
                     quantise(quant_at[s])
-                if is_tile(s - 2):
-                    regroup(s - 2)
                 if 0 <= s - NPAL and hh < NHEADS and r == 0:
                     q_regroup(hh)
                 if s in mx_at:

@@ -75,12 +75,15 @@ def tile_palaceattention_kernel(tc, x, inter_palace_weight, out):
         group_of = {}
         quant_at = {}
         mx_at = {}
+        divide_at = {}
         for n, tiles in enumerate(groups):
             for pos, i in enumerate(tiles):
                 group_of[i] = (n, pos)
             step = tiles[-1] + 2
             quant_at[step] = n
-            mx_at[step + 1] = n
+            mx_at[step + 1] = tiles
+            if tiles[-1] % QUAD == QUAD - 1:
+                divide_at[step + 2] = tiles[-1] // QUAD
 
         def q_transposes(hh):
             b, h = divmod(hh, H)
@@ -112,27 +115,25 @@ def tile_palaceattention_kernel(tc, x, inter_palace_weight, out):
             st[("qc", hh)] = qc
             st[("qs", hh)] = qs
 
-        def scores(i):
+        def scores(i, bank):
             hh, own = divmod(i, NPAL)
             qt = st[("qt", hh)]
             lhs = qt[:, own * P:(own + 1) * P]
-            s_a = ps_s.tile([P, BANK], FP32, tag="s_a")
-            s_b = ps_s.tile([P, BANK], FP32, tag="s_b")
-            for bank, dst in ((0, s_a), (1, s_b)):
-                first = (first_palace(own) + BANK_PALACES * bank) % NPAL
-                n1 = min(BANK_PALACES, NPAL - first)
-                nc.tensor.matmul(dst[:, 0:n1 * P], lhsT=lhs, rhs=qt[:, first * P:(first + n1) * P],
+            s_ps = ps_s.tile([P, BANK], FP32, tag="s%d" % bank)
+            first = (first_palace(own) + BANK_PALACES * bank) % NPAL
+            n1 = min(BANK_PALACES, NPAL - first)
+            nc.tensor.matmul(s_ps[:, 0:n1 * P], lhsT=lhs, rhs=qt[:, first * P:(first + n1) * P],
+                             start=True, stop=True)
+            if n1 < BANK_PALACES:
+                nc.tensor.matmul(s_ps[:, n1 * P:BANK], lhsT=lhs, rhs=qt[:, 0:(BANK_PALACES - n1) * P],
                                  start=True, stop=True)
-                if n1 < BANK_PALACES:
-                    nc.tensor.matmul(dst[:, n1 * P:BANK], lhsT=lhs, rhs=qt[:, 0:(BANK_PALACES - n1) * P],
-                                     start=True, stop=True)
-            st[("s", i)] = (s_a, s_b)
+            st[("s", i, bank)] = s_ps
 
         def own_columns(i):
             return slice(0, P) if i % 2 == 0 else slice(BANK - P, BANK)
 
         def scale_own(i):
-            s_a = st[("s", i)][0]
+            s_a = st[("s", i, 0)]
             sm = deep.tile([P, T], FP32, tag="sm")
             acc = deep.tile([P, 4], FP32, tag="acc")
             cols = own_columns(i)
@@ -142,14 +143,14 @@ def tile_palaceattention_kernel(tc, x, inter_palace_weight, out):
             st[("acc", i)] = acc
 
         def scale_rest_of_bank(i):
-            s_a = st[("s", i)][0]
+            s_a = st[("s", i, 0)]
             acc = st[("acc", i)]
             cols = slice(P, BANK) if i % 2 == 0 else slice(0, BANK - P)
             nc.vector.tensor_scalar(out=st[("sm", i)][:, cols], in0=s_a[:, cols], scalar1=ncsig[:, 0:1],
                                     scalar2=acc[:, 0:1], op0=ALU.mult, op1=ALU.min, accum_out=acc[:, 1:2])
 
         def scale_second_bank(i):
-            s_b = st[("s", i)][1]
+            s_b = st[("s", i, 1)]
             acc = st[("acc", i)]
             nc.vector.tensor_scalar(out=st[("sm", i)][:, BANK:T], in0=s_b[:], scalar1=ncsig[:, 0:1],
                                     scalar2=acc[:, 1:2], op0=ALU.mult, op1=ALU.min, accum_out=acc[:, 2:3])
@@ -200,34 +201,36 @@ def tile_palaceattention_kernel(tc, x, inter_palace_weight, out):
             st[("ec", n)] = ec
             st[("es", n)] = es
 
-        def multiply(n):
+        def multiply(i):
+            n, pos = group_of[i]
             ec, es = st[("ec", n)], st[("es", n)]
-            for pos, i in enumerate(groups[n]):
-                j, k = divmod(i, QUAD)
-                if k == 0:
-                    o_ps = ps_1.tile([P, QUAD, HD], FP32, tag="o_ps")
-                    st[("o_ps", j)] = o_ps
-                qc, qs = st[("qc", i // NPAL)], st[("qs", i // NPAL)]
-                for g in range(PASSES):
-                    ecols = slice((PASSES * pos + g) * P, (PASSES * pos + g + 1) * P)
-                    qcols = slice(g * HD, (g + 1) * HD)
-                    nc.tensor.matmul_mx(
-                        out=st[("o_ps", j)][:, k, :],
-                        lhsT=ec[:, ecols].bitcast(FP8X4),
-                        lhsT_scale=es[:, ecols],
-                        rhs=qc[:, qcols].bitcast(FP8X4),
-                        rhs_scale=qs[:, qcols],
-                        start=(g == 0),
-                        stop=(g == PASSES - 1),
-                    )
-                if k == QUAD - 1:
-                    divide_and_store(j)
+            j, k = divmod(i, QUAD)
+            if k == 0:
+                o_ps = ps_1.tile([P, QUAD, HD], FP32, tag="o_ps")
+                st[("o_ps", j)] = o_ps
+            qc, qs = st[("qc", i // NPAL)], st[("qs", i // NPAL)]
+            for g in range(PASSES):
+                ecols = slice((PASSES * pos + g) * P, (PASSES * pos + g + 1) * P)
+                qcols = slice(g * HD, (g + 1) * HD)
+                nc.tensor.matmul_mx(
+                    out=st[("o_ps", j)][:, k, :],
+                    lhsT=ec[:, ecols].bitcast(FP8X4),
+                    lhsT_scale=es[:, ecols],
+                    rhs=qc[:, qcols].bitcast(FP8X4),
+                    rhs_scale=qs[:, qcols],
+                    start=(g == 0),
+                    stop=(g == PASSES - 1),
+                )
+
+        def invert_row_sums(j):
+            rinv = deep.tile([P, QUAD], FP32, tag="rinv")
+            nc.vector.reciprocal(out=rinv[:], in_=st[("rs", j)][:])
+            st[("rinv", j)] = rinv
 
         def divide_and_store(j):
             hh, half = divmod(j, NPAL // QUAD)
             b, h = divmod(hh, H)
-            rinv = deep.tile([P, QUAD], FP32, tag="rinv")
-            nc.vector.reciprocal(out=rinv[:], in_=st[("rs", j)][:])
+            rinv = st[("rinv", j)]
             o_sb = work.tile([P, QUAD, HD], FP32, tag="o_sb")
             nc.vector.tensor_tensor(out=o_sb[:], in0=st[("o_ps", j)][:],
                                     in1=rinv[:].unsqueeze(2).to_broadcast([P, QUAD, HD]), op=ALU.mult)
@@ -243,36 +246,42 @@ def tile_palaceattention_kernel(tc, x, inter_palace_weight, out):
             nc.scalar.activation(out=warm[:], in_=sig[:], func=ACTF.Exp)
             q_regroup(0)
             q_quantise(0)
-            for s in range(-LEAD - 1, max(mx_at) + 1):
+            for s in range(-LEAD - 1, max(divide_at) + 1):
                 hh, r = divmod(s, NPAL)
                 following_head = hh + 1
                 head_follows = 0 <= s and following_head < NHEADS
                 if is_tile(s - 1):
                     e_transposes(s - 1)
                 if is_tile(s + LEAD + 1):
-                    scores(s + LEAD + 1)
+                    scores(s + LEAD + 1, 0)
+                for i in mx_at.get(s, ()):
+                    multiply(i)
+                if is_tile(s + LEAD + 1):
+                    scores(s + LEAD + 1, 1)
                 if head_follows and r == 1:
                     q_transposes(following_head)
                 if s + LEAD == -1:
                     scale_own(0)
                 if is_tile(s + LEAD):
                     scale_rest_of_bank(s + LEAD)
+                if s in quant_at:
+                    next_tile = groups[quant_at[s]][-1] + 1
+                    if next_tile % NPAL == 0 and next_tile < NTILES:
+                        q_quantise(next_tile // NPAL)
+                    quantise(quant_at[s])
+                if s in divide_at:
+                    divide_and_store(divide_at[s])
                 if is_tile(s + LEAD) and is_tile(s + LEAD + 1):
                     scale_own(s + LEAD + 1)
                 if is_tile(s + LEAD):
                     scale_second_bank(s + LEAD)
+                if is_tile(s - 2) and s % QUAD == 1:
+                    invert_row_sums((s - 2) // QUAD)
                 if is_tile(s):
                     exponential(s)
                 if is_tile(s - 1):
                     copy_out(s - 1)
                 if head_follows and r == 2:
                     q_copy(following_head)
-                if s in quant_at:
-                    next_tile = groups[quant_at[s]][-1] + 1
-                    if next_tile % NPAL == 0 and next_tile < NTILES:
-                        q_quantise(next_tile // NPAL)
-                    quantise(quant_at[s])
                 if 0 <= s - NPAL and hh < NHEADS and r == 0:
                     q_regroup(hh)
-                if s in mx_at:
-                    multiply(mx_at[s])

@@ -33,6 +33,10 @@ def first_palace(own):
     return own if own % 2 == 0 else (own - BANK_PALACES + 1) % NPAL
 
 
+def scalar_divides(j):
+    return j % 2 == 1 and j < NTILES // QUAD - 1
+
+
 def tile_groups():
     groups = [tuple(range(QUAD * j, QUAD * j + QUAD)) for j in range(NTILES // QUAD - 1)]
     return groups + [(TAIL, TAIL + 1), (TAIL + 2,), (TAIL + 3,)]
@@ -232,8 +236,13 @@ def tile_palaceattention_kernel(tc, x, inter_palace_weight, out):
             b, h = divmod(hh, H)
             rinv = st[("rinv", j)]
             o_sb = work.tile([P, QUAD, HD], FP32, tag="o_sb")
-            nc.vector.tensor_tensor(out=o_sb[:], in0=st[("o_ps", j)][:],
-                                    in1=rinv[:].unsqueeze(2).to_broadcast([P, QUAD, HD]), op=ALU.mult)
+            if scalar_divides(j):
+                for k in range(QUAD):
+                    nc.scalar.activation(out=o_sb[:, k, :], in_=st[("o_ps", j)][:, k, :], func=ACTF.Copy,
+                                         scale=rinv[:, k:k + 1])
+            else:
+                nc.vector.tensor_tensor(out=o_sb[:], in0=st[("o_ps", j)][:],
+                                        in1=rinv[:].unsqueeze(2).to_broadcast([P, QUAD, HD]), op=ALU.mult)
             nc.sync.dma_start(out=ov[b][:, half * QUAD:(half + 1) * QUAD, h * HD:(h + 1) * HD], in_=o_sb[:])
 
         def is_tile(i):
@@ -269,7 +278,7 @@ def tile_palaceattention_kernel(tc, x, inter_palace_weight, out):
                     if next_tile % NPAL == 0 and next_tile < NTILES:
                         q_quantise(next_tile // NPAL)
                     quantise(quant_at[s])
-                if s in divide_at:
+                if s in divide_at and not scalar_divides(divide_at[s]):
                     divide_and_store(divide_at[s])
                 if is_tile(s + LEAD) and is_tile(s + LEAD + 1):
                     scale_own(s + LEAD + 1)
@@ -279,6 +288,8 @@ def tile_palaceattention_kernel(tc, x, inter_palace_weight, out):
                     invert_row_sums((s - 2) // QUAD)
                 if is_tile(s):
                     exponential(s)
+                if s in divide_at and scalar_divides(divide_at[s]):
+                    divide_and_store(divide_at[s])
                 if is_tile(s - 1):
                     copy_out(s - 1)
                 if head_follows and r == 2:

@@ -25,15 +25,16 @@ SCALE = HD ** -0.5
 FLOPS = 2 * 2 * NB * H * T * T * HD
 
 LEAD = 2
+WARM_UP = 5
 TAIL = NTILES - QUAD
-LOADS = ((0, 0, 128), (0, 128, 256), (0, 256, 512), (0, 512, 1024), (1, 0, 512), (1, 512, 1024))
+LOADS = ((0, 128, 256), (0, 256, 512), (0, 512, 1024), (1, 0, 512), (1, 512, 1024))
 
 
 def first_palace(own):
     return own if own % 2 == 0 else (own - BANK_PALACES + 1) % NPAL
 
 
-def scalar_divides(j):
+def scalar_empties(j):
     return j % 2 == 1 and j < NTILES // QUAD - 1
 
 
@@ -58,13 +59,17 @@ def tile_palaceattention_kernel(tc, x, inter_palace_weight, out):
         ov = [out[b].rearrange("(a l) c -> a l c", l=NPAL) for b in range(NB)]
 
         w_bf = const.tile([P, 1], BF16)
-        nc.sync.dma_start(out=w_bf[:], in_=inter_palace_weight.partition_broadcast(P))
+        nc.scalar.dma_start(out=w_bf[:], in_=inter_palace_weight.partition_broadcast(P))
         x0 = const.tile([P, NPAL, H * HD], BF16)
         x1 = const.tile([P, NPAL, H * HD], BF16)
         xin = [x0, x1]
+        for l0 in (0, BANK_PALACES):
+            nc.sync.dma_start(out=x0[:, l0:l0 + BANK_PALACES, 0:HD], in_=xv[0][:, l0:l0 + BANK_PALACES, 0:HD])
         for b, c0, c1 in LOADS:
             nc.sync.dma_start(out=xin[b][:, :, c0:c1], in_=xv[b][:, :, c0:c1])
 
+        zeros = const.tile([P, BANK], BF16)
+        nc.vector.memset(zeros[:], 0.0)
         ident = const.tile([P, P], BF16)
         make_identity(nc, ident[:])
         ident_f32 = const.tile([P, P], FP32)
@@ -95,6 +100,19 @@ def tile_palaceattention_kernel(tc, x, inter_palace_weight, out):
             for pal in range(NPAL):
                 nc.tensor.transpose(pt[:, pal, :], xin[b][:, pal, h * HD:(h + 1) * HD], ident[:])
             st[("pt", hh)] = pt
+
+        def first_q():
+            qt = headp.tile([P, NPAL * P], BF16, tag="qt")
+            for l0 in (0, BANK_PALACES):
+                ph = ps_x.tile([P, BANK_PALACES, P], BF16, tag="xt")
+                for k in range(BANK_PALACES):
+                    nc.tensor.transpose(ph[:, k, :], xin[0][:, l0 + k, 0:HD], ident[:])
+                half = qt[:, l0 * P:(l0 + BANK_PALACES) * P]
+                if l0 == 0:
+                    nc.scalar.copy(out=half, in_=ph[:].rearrange("p l y -> p (l y)"))
+                else:
+                    nc.vector.tensor_copy(out=half, in_=ph[:].rearrange("p l y -> p (l y)"))
+            st[("qt", 0)] = qt
 
         def q_copy(hh):
             qt = headp.tile([P, NPAL * P], BF16, tag="qt")
@@ -188,7 +206,7 @@ def tile_palaceattention_kernel(tc, x, inter_palace_weight, out):
             n, pos = group_of[i]
             dst = grouped_tile(n)[:, pos, :].bitcast(FP32).rearrange("p (g y u) -> p g y u", g=PASSES, u=2)
             src = st[("xt", i)][:].rearrange("p (g u) y -> p g y u", u=2)
-            if i >= TAIL and i % 2 == 0:
+            if i in (TAIL + 1, TAIL + 2):
                 nc.vector.tensor_copy(out=dst, in_=src)
             else:
                 nc.scalar.copy(out=dst, in_=src)
@@ -212,12 +230,16 @@ def tile_palaceattention_kernel(tc, x, inter_palace_weight, out):
             if k == 0:
                 o_ps = ps_1.tile([P, QUAD, HD], FP32, tag="o_ps")
                 st[("o_ps", j)] = o_ps
+            o_ps = st[("o_ps", j)]
+            if i == NTILES - 1:
+                o_last = ps_1.tile([P, QUAD, HD], FP32, tag="pt")
+                o_ps = st[("o_ps", "last")] = o_last
             qc, qs = st[("qc", i // NPAL)], st[("qs", i // NPAL)]
             for g in range(PASSES):
                 ecols = slice((PASSES * pos + g) * P, (PASSES * pos + g + 1) * P)
                 qcols = slice(g * HD, (g + 1) * HD)
                 nc.tensor.matmul_mx(
-                    out=st[("o_ps", j)][:, k, :],
+                    out=o_ps[:, k, :],
                     lhsT=ec[:, ecols].bitcast(FP8X4),
                     lhsT_scale=es[:, ecols],
                     rhs=qc[:, qcols].bitcast(FP8X4),
@@ -236,25 +258,38 @@ def tile_palaceattention_kernel(tc, x, inter_palace_weight, out):
             b, h = divmod(hh, H)
             rinv = st[("rinv", j)]
             o_sb = work.tile([P, QUAD, HD], FP32, tag="o_sb")
-            if scalar_divides(j):
+            if scalar_empties(j):
+                o_raw = work.tile([P, QUAD, HD], FP32, tag="o_raw")
+                nc.scalar.copy(out=o_raw[:], in_=st[("o_ps", j)][:])
                 for k in range(QUAD):
-                    nc.scalar.activation(out=o_sb[:, k, :], in_=st[("o_ps", j)][:, k, :], func=ACTF.Copy,
-                                         scale=rinv[:, k:k + 1])
+                    nc.gpsimd.tensor_scalar(out=o_sb[:, k, :], in0=o_raw[:, k, :], scalar1=rinv[:, k:k + 1],
+                                            scalar2=0.0, op0=ALU.mult, op1=ALU.add)
             else:
                 nc.vector.tensor_tensor(out=o_sb[:], in0=st[("o_ps", j)][:],
                                         in1=rinv[:].unsqueeze(2).to_broadcast([P, QUAD, HD]), op=ALU.mult)
             nc.sync.dma_start(out=ov[b][:, half * QUAD:(half + 1) * QUAD, h * HD:(h + 1) * HD], in_=o_sb[:])
 
+        def divide_and_store_last():
+            j = NTILES // QUAD - 1
+            rinv = st[("rinv", j)]
+            o_sb = work.tile([P, QUAD, HD], FP32, tag="o_sb")
+            for k0, k1, o_ps in ((0, QUAD - 1, st[("o_ps", j)]), (QUAD - 1, QUAD, st[("o_ps", "last")])):
+                nc.vector.tensor_tensor(out=o_sb[:, k0:k1, :], in0=o_ps[:, k0:k1, :],
+                                        in1=rinv[:, k0:k1].unsqueeze(2).to_broadcast([P, k1 - k0, HD]), op=ALU.mult)
+                nc.sync.dma_start(out=ov[NB - 1][:, NPAL - QUAD + k0:NPAL - QUAD + k1, (H - 1) * HD:H * HD],
+                                  in_=o_sb[:, k0:k1, :])
+
         def is_tile(i):
             return 0 <= i < NTILES
 
         with tc.manual_schedule():
-            q_transposes(0)
-            q_copy(0)
+            idle = ps_1.tile([P, BANK], FP32, tag="o_ps")
+            for k in range(WARM_UP):
+                nc.tensor.matmul(idle[:], lhsT=zeros[:, 0:P], rhs=zeros[:], start=True, stop=True)
+            first_q()
             warm = const.tile([P, 1], FP32)
             nc.scalar.activation(out=warm[:], in_=sig[:], func=ACTF.Exp)
             q_regroup(0)
-            q_quantise(0)
             for s in range(-LEAD - 1, max(divide_at) + 1):
                 hh, r = divmod(s, NPAL)
                 following_head = hh + 1
@@ -271,24 +306,27 @@ def tile_palaceattention_kernel(tc, x, inter_palace_weight, out):
                     q_transposes(following_head)
                 if s + LEAD == -1:
                     scale_own(0)
+                    q_quantise(0)
                 if is_tile(s + LEAD):
                     scale_rest_of_bank(s + LEAD)
+                if is_tile(s - 2) and s % QUAD == 1:
+                    invert_row_sums((s - 2) // QUAD)
                 if s in quant_at:
                     next_tile = groups[quant_at[s]][-1] + 1
                     if next_tile % NPAL == 0 and next_tile < NTILES:
                         q_quantise(next_tile // NPAL)
                     quantise(quant_at[s])
-                if s in divide_at and not scalar_divides(divide_at[s]):
+                if s == max(divide_at):
+                    divide_and_store_last()
+                elif s in divide_at and not scalar_empties(divide_at[s]):
                     divide_and_store(divide_at[s])
                 if is_tile(s + LEAD) and is_tile(s + LEAD + 1):
                     scale_own(s + LEAD + 1)
                 if is_tile(s + LEAD):
                     scale_second_bank(s + LEAD)
-                if is_tile(s - 2) and s % QUAD == 1:
-                    invert_row_sums((s - 2) // QUAD)
                 if is_tile(s):
                     exponential(s)
-                if s in divide_at and scalar_divides(divide_at[s]):
+                if s in divide_at and scalar_empties(divide_at[s]):
                     divide_and_store(divide_at[s])
                 if is_tile(s - 1):
                     copy_out(s - 1)

@@ -34,8 +34,8 @@ def first_palace(own):
     return own if own % 2 == 0 else (own - BANK_PALACES + 1) % NPAL
 
 
-def scalar_empties(j):
-    return j % 2 == 1 and j < NTILES // QUAD - 1
+def scalar_divides(j):
+    return j % 3 == 1 and j < NTILES // QUAD - 1
 
 
 def tile_groups():
@@ -258,12 +258,10 @@ def tile_palaceattention_kernel(tc, x, inter_palace_weight, out):
             b, h = divmod(hh, H)
             rinv = st[("rinv", j)]
             o_sb = work.tile([P, QUAD, HD], FP32, tag="o_sb")
-            if scalar_empties(j):
-                o_raw = work.tile([P, QUAD, HD], FP32, tag="o_raw")
-                nc.scalar.copy(out=o_raw[:], in_=st[("o_ps", j)][:])
+            if scalar_divides(j):
                 for k in range(QUAD):
-                    nc.gpsimd.tensor_scalar(out=o_sb[:, k, :], in0=o_raw[:, k, :], scalar1=rinv[:, k:k + 1],
-                                            scalar2=0.0, op0=ALU.mult, op1=ALU.add)
+                    nc.scalar.activation(out=o_sb[:, k, :], in_=st[("o_ps", j)][:, k, :], func=ACTF.Copy,
+                                         scale=rinv[:, k:k + 1])
             else:
                 nc.vector.tensor_tensor(out=o_sb[:], in0=st[("o_ps", j)][:],
                                         in1=rinv[:].unsqueeze(2).to_broadcast([P, QUAD, HD]), op=ALU.mult)
@@ -309,8 +307,6 @@ def tile_palaceattention_kernel(tc, x, inter_palace_weight, out):
                     q_quantise(0)
                 if is_tile(s + LEAD):
                     scale_rest_of_bank(s + LEAD)
-                if is_tile(s - 2) and s % QUAD == 1:
-                    invert_row_sums((s - 2) // QUAD)
                 if s in quant_at:
                     next_tile = groups[quant_at[s]][-1] + 1
                     if next_tile % NPAL == 0 and next_tile < NTILES:
@@ -318,15 +314,17 @@ def tile_palaceattention_kernel(tc, x, inter_palace_weight, out):
                     quantise(quant_at[s])
                 if s == max(divide_at):
                     divide_and_store_last()
-                elif s in divide_at and not scalar_empties(divide_at[s]):
+                elif s in divide_at and not scalar_divides(divide_at[s]):
                     divide_and_store(divide_at[s])
                 if is_tile(s + LEAD) and is_tile(s + LEAD + 1):
                     scale_own(s + LEAD + 1)
                 if is_tile(s + LEAD):
                     scale_second_bank(s + LEAD)
+                if is_tile(s - 2) and s % QUAD == 1:
+                    invert_row_sums((s - 2) // QUAD)
                 if is_tile(s):
                     exponential(s)
-                if s in divide_at and scalar_empties(divide_at[s]):
+                if s in divide_at and scalar_divides(divide_at[s]):
                     divide_and_store(divide_at[s])
                 if is_tile(s - 1):
                     copy_out(s - 1)

@@ -70,6 +70,8 @@ def tile_palaceattention_kernel(tc, x, inter_palace_weight, out):
 
         zeros = const.tile([P, BANK], BF16)
         nc.vector.memset(zeros[:], 0.0)
+        minus_one = const.tile([P, QUAD], FP32)
+        nc.gpsimd.memset(minus_one[:], -1.0)
         ident = const.tile([P, P], BF16)
         make_identity(nc, ident[:])
         ident_f32 = const.tile([P, P], FP32)
@@ -119,12 +121,14 @@ def tile_palaceattention_kernel(tc, x, inter_palace_weight, out):
             nc.scalar.copy(out=qt[:], in_=st[("pt", hh)][:].rearrange("p l y -> p (l y)"))
             st[("qt", hh)] = qt
 
-        def q_regroup(hh):
+        def q_regroup(hh, g):
             b, h = divmod(hh, H)
-            qg = headp.tile([P, PASSES, HD, PACK], BF16, tag="qg", align_bytes=64)
-            src = xin[b][:, :, h * HD:(h + 1) * HD].rearrange("p (g t) d -> p g d t", t=PACK)
-            nc.gpsimd.tensor_scalar(out=qg[:], in0=src, scalar1=1.0, scalar2=0.0, op0=ALU.mult, op1=ALU.add)
-            st[("qg", hh)] = qg
+            if g == 0:
+                qg = headp.tile([P, PASSES, HD, PACK], BF16, tag="qg", align_bytes=64)
+                st[("qg", hh)] = qg
+            src = xin[b][:, PACK * g:PACK * (g + 1), h * HD:(h + 1) * HD].rearrange("p t d -> p d t")
+            nc.gpsimd.tensor_scalar(out=st[("qg", hh)][:, g], in0=src, scalar1=1.0, scalar2=0.0,
+                                    op0=ALU.mult, op1=ALU.add)
 
         def q_quantise(hh):
             qc = headp.tile([P, PASSES * HD], U32, tag="qc", align_bytes=64)
@@ -250,7 +254,7 @@ def tile_palaceattention_kernel(tc, x, inter_palace_weight, out):
 
         def invert_row_sums(j):
             rinv = deep.tile([P, QUAD], FP32, tag="rinv")
-            nc.vector.reciprocal(out=rinv[:], in_=st[("rs", j)][:])
+            nc.gpsimd.tensor_tensor(out=rinv[:], in0=st[("rs", j)][:], in1=minus_one[:], op=ALU.pow)
             st[("rinv", j)] = rinv
 
         def divide_and_store(j):
@@ -287,11 +291,12 @@ def tile_palaceattention_kernel(tc, x, inter_palace_weight, out):
             first_q()
             warm = const.tile([P, 1], FP32)
             nc.scalar.activation(out=warm[:], in_=sig[:], func=ACTF.Exp)
-            q_regroup(0)
+            for g in range(PASSES):
+                q_regroup(0, g)
             for s in range(-LEAD - 1, max(divide_at) + 1):
                 hh, r = divmod(s, NPAL)
                 following_head = hh + 1
-                head_follows = 0 <= s and following_head < NHEADS
+                head_follows = 1 <= hh and following_head < NHEADS
                 if is_tile(s - 1):
                     e_transposes(s - 1)
                 if is_tile(s + LEAD + 1):
@@ -302,6 +307,9 @@ def tile_palaceattention_kernel(tc, x, inter_palace_weight, out):
                     scores(s + LEAD + 1, 1)
                 if head_follows and r == 1:
                     q_transposes(following_head)
+                if s == -LEAD:
+                    q_transposes(1)
+                    q_copy(1)
                 if s + LEAD == -1:
                     scale_own(0)
                     q_quantise(0)
@@ -322,6 +330,10 @@ def tile_palaceattention_kernel(tc, x, inter_palace_weight, out):
                     scale_second_bank(s + LEAD)
                 if is_tile(s - 2) and s % QUAD == 1:
                     invert_row_sums((s - 2) // QUAD)
+                    j = (s - 2) // QUAD
+                    for half in (2, 3) if j == 0 else (j + 3,):
+                        if half < PASSES * NHEADS:
+                            q_regroup(*divmod(half, PASSES))
                 if is_tile(s):
                     exponential(s)
                 if s in divide_at and scalar_divides(divide_at[s]):
@@ -330,5 +342,3 @@ def tile_palaceattention_kernel(tc, x, inter_palace_weight, out):
                     copy_out(s - 1)
                 if head_follows and r == 2:
                     q_copy(following_head)
-                if 0 <= s - NPAL and hh < NHEADS and r == 0:
-                    q_regroup(hh)

from contextlib import ExitStack

import concourse.mybir as mybir
from concourse.masks import make_identity

FP32 = mybir.dt.float32
BF16 = mybir.dt.bfloat16
U32 = mybir.dt.uint32
U8 = mybir.dt.uint8
FP8X4 = mybir.dt.float8_e4m3fn_x4
ALU = mybir.AluOpType
ACTF = mybir.ActivationFunctionType

NB, T, H, HD = 2, 1024, 8, 128
NPAL = 8
P = 128
PACK = 4
PASSES = T // (P * PACK)
BANK = 512
BANK_PALACES = BANK // P
NHEADS = NB * H
NTILES = NHEADS * NPAL
QUAD = 4
SCALE = HD ** -0.5
FLOPS = 2 * 2 * NB * H * T * T * HD

LEAD = 2
WARM_UP = 5
TAIL = NTILES - QUAD
LOADS = ((0, 128, 256), (0, 256, 512), (0, 512, 1024), (1, 0, 512), (1, 512, 1024))


def first_palace(own):
    return own if own % 2 == 0 else (own - BANK_PALACES + 1) % NPAL


def scalar_divides(j):
    return j % 3 == 1 and j < NTILES // QUAD - 1


def tile_groups():
    groups = [tuple(range(QUAD * j, QUAD * j + QUAD)) for j in range(NTILES // QUAD - 1)]
    return groups + [(TAIL, TAIL + 1), (TAIL + 2,), (TAIL + 3,)]


def tile_palaceattention_kernel(tc, x, inter_palace_weight, out):
    nc = tc.nc
    with ExitStack() as ctx:
        const = ctx.enter_context(tc.tile_pool(name="const", bufs=1))
        headp = ctx.enter_context(tc.tile_pool(name="headp", bufs=2))
        work = ctx.enter_context(tc.tile_pool(name="work", bufs=3))
        deep = ctx.enter_context(tc.tile_pool(name="deep", bufs=4))
        grp = ctx.enter_context(tc.tile_pool(name="grp", bufs=2))
        ps_s = ctx.enter_context(tc.psum_pool(name="ps_s", bufs=2))
        ps_x = ctx.enter_context(tc.psum_pool(name="ps_x", bufs=2))
        ps_1 = ctx.enter_context(tc.psum_pool(name="ps_1", bufs=1))

        xv = [x[b].rearrange("(a l) c -> a l c", l=NPAL) for b in range(NB)]
        ov = [out[b].rearrange("(a l) c -> a l c", l=NPAL) for b in range(NB)]

        w_bf = const.tile([P, 1], BF16)
        nc.scalar.dma_start(out=w_bf[:], in_=inter_palace_weight.partition_broadcast(P))
        x0 = const.tile([P, NPAL, H * HD], BF16)
        x1 = const.tile([P, NPAL, H * HD], BF16)
        xin = [x0, x1]
        for l0 in (0, BANK_PALACES):
            nc.sync.dma_start(out=x0[:, l0:l0 + BANK_PALACES, 0:HD], in_=xv[0][:, l0:l0 + BANK_PALACES, 0:HD])
        for b, c0, c1 in LOADS:
            nc.sync.dma_start(out=xin[b][:, :, c0:c1], in_=xv[b][:, :, c0:c1])

        zeros = const.tile([P, BANK], BF16)
        nc.vector.memset(zeros[:], 0.0)
        minus_one = const.tile([P, QUAD], FP32)
        nc.gpsimd.memset(minus_one[:], -1.0)
        ident = const.tile([P, P], BF16)
        make_identity(nc, ident[:])
        ident_f32 = const.tile([P, P], FP32)
        make_identity(nc, ident_f32[:])
        sig = const.tile([P, 1], FP32)
        nc.scalar.activation(out=sig[:], in_=w_bf[:], func=ACTF.Sigmoid)
        ncsig = const.tile([P, 1], FP32)
        nc.vector.tensor_scalar(out=ncsig[:], in0=sig[:], scalar1=-SCALE, scalar2=None, op0=ALU.mult)

        st = {}
        groups = tile_groups()
        group_of = {}
        quant_at = {}
        mx_at = {}
        divide_at = {}
        for n, tiles in enumerate(groups):
            for pos, i in enumerate(tiles):
                group_of[i] = (n, pos)
            step = tiles[-1] + 2
            quant_at[step] = n
            mx_at[step + 1] = tiles
            if tiles[-1] % QUAD == QUAD - 1:
                divide_at[step + 2] = tiles[-1] // QUAD

        def q_transposes(hh):
            b, h = divmod(hh, H)
            pt = ps_1.tile([P, NPAL, P], BF16, tag="pt")
            for pal in range(NPAL):
                nc.tensor.transpose(pt[:, pal, :], xin[b][:, pal, h * HD:(h + 1) * HD], ident[:])
            st[("pt", hh)] = pt

        def first_q():
            qt = headp.tile([P, NPAL * P], BF16, tag="qt")
            for l0 in (0, BANK_PALACES):
                ph = ps_x.tile([P, BANK_PALACES, P], BF16, tag="xt")
                for k in range(BANK_PALACES):
                    nc.tensor.transpose(ph[:, k, :], xin[0][:, l0 + k, 0:HD], ident[:])
                half = qt[:, l0 * P:(l0 + BANK_PALACES) * P]
                if l0 == 0:
                    nc.scalar.copy(out=half, in_=ph[:].rearrange("p l y -> p (l y)"))
                else:
                    nc.vector.tensor_copy(out=half, in_=ph[:].rearrange("p l y -> p (l y)"))
            st[("qt", 0)] = qt

        def q_copy(hh):
            qt = headp.tile([P, NPAL * P], BF16, tag="qt")
            nc.scalar.copy(out=qt[:], in_=st[("pt", hh)][:].rearrange("p l y -> p (l y)"))
            st[("qt", hh)] = qt

        def q_regroup(hh, g):
            b, h = divmod(hh, H)
            if g == 0:
                qg = headp.tile([P, PASSES, HD, PACK], BF16, tag="qg", align_bytes=64)
                st[("qg", hh)] = qg
            src = xin[b][:, PACK * g:PACK * (g + 1), h * HD:(h + 1) * HD].rearrange("p t d -> p d t")
            nc.gpsimd.tensor_scalar(out=st[("qg", hh)][:, g], in0=src, scalar1=1.0, scalar2=0.0,
                                    op0=ALU.mult, op1=ALU.add)

        def q_quantise(hh):
            qc = headp.tile([P, PASSES * HD], U32, tag="qc", align_bytes=64)
            qs = headp.tile([P, PASSES * HD], U8, tag="qs", align_bytes=64)
            nc.vector.quantize_mx(
                out=qc[:].bitcast(FP8X4),
                scales=qs[:],
                in_=st[("qg", hh)][:].rearrange("p g d t -> p (g d t)"),
            )
            st[("qc", hh)] = qc
            st[("qs", hh)] = qs

        def scores(i, bank):
            hh, own = divmod(i, NPAL)
            qt = st[("qt", hh)]
            lhs = qt[:, own * P:(own + 1) * P]
            s_ps = ps_s.tile([P, BANK], FP32, tag="s%d" % bank)
            first = (first_palace(own) + BANK_PALACES * bank) % NPAL
            n1 = min(BANK_PALACES, NPAL - first)
            nc.tensor.matmul(s_ps[:, 0:n1 * P], lhsT=lhs, rhs=qt[:, first * P:(first + n1) * P],
                             start=True, stop=True)
            if n1 < BANK_PALACES:
                nc.tensor.matmul(s_ps[:, n1 * P:BANK], lhsT=lhs, rhs=qt[:, 0:(BANK_PALACES - n1) * P],
                                 start=True, stop=True)
            st[("s", i, bank)] = s_ps

        def own_columns(i):
            return slice(0, P) if i % 2 == 0 else slice(BANK - P, BANK)

        def scale_own(i):
            s_a = st[("s", i, 0)]
            sm = deep.tile([P, T], FP32, tag="sm")
            acc = deep.tile([P, 4], FP32, tag="acc")
            cols = own_columns(i)
            nc.vector.tensor_scalar(out=sm[:, cols], in0=s_a[:, cols], scalar1=-SCALE, scalar2=None,
                                    op0=ALU.mult, op1=ALU.min, accum_out=acc[:, 0:1])
            st[("sm", i)] = sm
            st[("acc", i)] = acc

        def scale_rest_of_bank(i):
            s_a = st[("s", i, 0)]
            acc = st[("acc", i)]
            cols = slice(P, BANK) if i % 2 == 0 else slice(0, BANK - P)
            nc.vector.tensor_scalar(out=st[("sm", i)][:, cols], in0=s_a[:, cols], scalar1=ncsig[:, 0:1],
                                    scalar2=acc[:, 0:1], op0=ALU.mult, op1=ALU.min, accum_out=acc[:, 1:2])

        def scale_second_bank(i):
            s_b = st[("s", i, 1)]
            acc = st[("acc", i)]
            nc.vector.tensor_scalar(out=st[("sm", i)][:, BANK:T], in0=s_b[:], scalar1=ncsig[:, 0:1],
                                    scalar2=acc[:, 1:2], op0=ALU.mult, op1=ALU.min, accum_out=acc[:, 2:3])

        def exponential(i):
            j, k = divmod(i, QUAD)
            if k == 0:
                rs = deep.tile([P, QUAD], FP32, tag="rs")
                st[("rs", j)] = rs
            e = work.tile([P, T], BF16, tag="e")
            nc.scalar.activation(out=e[:].rearrange("p (u a e) -> p u a e", a=P, e=2),
                                 in_=st[("sm", i)][:].rearrange("p (u e a) -> p u a e", a=P, e=2), func=ACTF.Exp, bias=st[("acc", i)][:, 2:3],
                                 scale=-1.0, accum_out=st[("rs", j)][:, k:k + 1])
            st[("e", i)] = e

        def e_transposes(i):
            first = first_palace(i % NPAL) // 2
            words = st[("e", i)][:].bitcast(FP32)
            xt = ps_x.tile([P, NPAL // 2, P], FP32, tag="xt")
            for u in range(NPAL // 2):
                nc.tensor.transpose(xt[:, (first + u) % (NPAL // 2), :], words[:, u * P:(u + 1) * P], ident_f32[:])
            st[("xt", i)] = xt

        def grouped_tile(n):
            if ("gr", n) not in st:
                gr = grp.tile([P, len(groups[n]), PASSES * P * PACK], BF16, tag="gr%d" % len(groups[n]), align_bytes=64)
                st[("gr", n)] = gr
            return st[("gr", n)]

        def copy_out(i):
            n, pos = group_of[i]
            dst = grouped_tile(n)[:, pos, :].bitcast(FP32).rearrange("p (g y u) -> p g y u", g=PASSES, u=2)
            src = st[("xt", i)][:].rearrange("p (g u) y -> p g y u", u=2)
            if i in (TAIL + 1, TAIL + 2):
                nc.vector.tensor_copy(out=dst, in_=src)
            else:
                nc.scalar.copy(out=dst, in_=src)

        def quantise(n):
            width = PASSES * P * len(groups[n])
            ec = headp.tile([P, width], U32, tag="ec", align_bytes=64)
            es = headp.tile([P, width], U8, tag="es", align_bytes=64)
            nc.vector.quantize_mx(
                out=ec[:].bitcast(FP8X4),
                scales=es[:],
                in_=st[("gr", n)][:].rearrange("p i k -> p (i k)"),
            )
            st[("ec", n)] = ec
            st[("es", n)] = es

        def multiply(i):
            n, pos = group_of[i]
            ec, es = st[("ec", n)], st[("es", n)]
            j, k = divmod(i, QUAD)
            if k == 0:
                o_ps = ps_1.tile([P, QUAD, HD], FP32, tag="o_ps")
                st[("o_ps", j)] = o_ps
            o_ps = st[("o_ps", j)]
            if i == NTILES - 1:
                o_last = ps_1.tile([P, QUAD, HD], FP32, tag="pt")
                o_ps = st[("o_ps", "last")] = o_last
            qc, qs = st[("qc", i // NPAL)], st[("qs", i // NPAL)]
            for g in range(PASSES):
                ecols = slice((PASSES * pos + g) * P, (PASSES * pos + g + 1) * P)
                qcols = slice(g * HD, (g + 1) * HD)
                nc.tensor.matmul_mx(
                    out=o_ps[:, k, :],
                    lhsT=ec[:, ecols].bitcast(FP8X4),
                    lhsT_scale=es[:, ecols],
                    rhs=qc[:, qcols].bitcast(FP8X4),
                    rhs_scale=qs[:, qcols],
                    start=(g == 0),
                    stop=(g == PASSES - 1),
                )

        def invert_row_sums(j):
            rinv = deep.tile([P, QUAD], FP32, tag="rinv")
            nc.gpsimd.tensor_tensor(out=rinv[:], in0=st[("rs", j)][:], in1=minus_one[:], op=ALU.pow)
            st[("rinv", j)] = rinv

        def divide_and_store(j):
            hh, half = divmod(j, NPAL // QUAD)
            b, h = divmod(hh, H)
            rinv = st[("rinv", j)]
            o_sb = work.tile([P, QUAD, HD], FP32, tag="o_sb")
            if scalar_divides(j):
                for k in range(QUAD):
                    nc.scalar.activation(out=o_sb[:, k, :], in_=st[("o_ps", j)][:, k, :], func=ACTF.Copy,
                                         scale=rinv[:, k:k + 1])
            else:
                nc.vector.tensor_tensor(out=o_sb[:], in0=st[("o_ps", j)][:],
                                        in1=rinv[:].unsqueeze(2).to_broadcast([P, QUAD, HD]), op=ALU.mult)
            nc.sync.dma_start(out=ov[b][:, half * QUAD:(half + 1) * QUAD, h * HD:(h + 1) * HD], in_=o_sb[:])

        def divide_and_store_last():
            j = NTILES // QUAD - 1
            rinv = st[("rinv", j)]
            o_sb = work.tile([P, QUAD, HD], FP32, tag="o_sb")
            for k0, k1, o_ps in ((0, QUAD - 1, st[("o_ps", j)]), (QUAD - 1, QUAD, st[("o_ps", "last")])):
                nc.vector.tensor_tensor(out=o_sb[:, k0:k1, :], in0=o_ps[:, k0:k1, :],
                                        in1=rinv[:, k0:k1].unsqueeze(2).to_broadcast([P, k1 - k0, HD]), op=ALU.mult)
                nc.sync.dma_start(out=ov[NB - 1][:, NPAL - QUAD + k0:NPAL - QUAD + k1, (H - 1) * HD:H * HD],
                                  in_=o_sb[:, k0:k1, :])

        def is_tile(i):
            return 0 <= i < NTILES

        with tc.manual_schedule():
            idle = ps_1.tile([P, BANK], FP32, tag="o_ps")
            for k in range(WARM_UP):
                nc.tensor.matmul(idle[:], lhsT=zeros[:, 0:P], rhs=zeros[:], start=True, stop=True)
            first_q()
            warm = const.tile([P, 1], FP32)
            nc.scalar.activation(out=warm[:], in_=sig[:], func=ACTF.Exp)
            for g in range(PASSES):
                q_regroup(0, g)
            for s in range(-LEAD - 1, max(divide_at) + 1):
                hh, r = divmod(s, NPAL)
                following_head = hh + 1
                head_follows = 1 <= hh and following_head < NHEADS
                if is_tile(s - 1):
                    e_transposes(s - 1)
                if is_tile(s + LEAD + 1):
                    scores(s + LEAD + 1, 0)
                for i in mx_at.get(s, ()):
                    multiply(i)
                if is_tile(s + LEAD + 1):
                    scores(s + LEAD + 1, 1)
                if head_follows and r == 1:
                    q_transposes(following_head)
                if s == -LEAD:
                    q_transposes(1)
                    q_copy(1)
                if s + LEAD == -1:
                    scale_own(0)
                    q_quantise(0)
                if is_tile(s + LEAD):
                    scale_rest_of_bank(s + LEAD)
                if s in quant_at:
                    next_tile = groups[quant_at[s]][-1] + 1
                    if next_tile % NPAL == 0 and next_tile < NTILES:
                        q_quantise(next_tile // NPAL)
                    quantise(quant_at[s])
                if s == max(divide_at):
                    divide_and_store_last()
                elif s in divide_at and not scalar_divides(divide_at[s]):
                    divide_and_store(divide_at[s])
                if is_tile(s + LEAD) and is_tile(s + LEAD + 1):
                    scale_own(s + LEAD + 1)
                if is_tile(s + LEAD):
                    scale_second_bank(s + LEAD)
                if is_tile(s - 2) and s % QUAD == 1:
                    invert_row_sums((s - 2) // QUAD)
                    j = (s - 2) // QUAD
                    for half in (2, 3) if j == 0 else (j + 3,):
                        if half < PASSES * NHEADS:
                            q_regroup(*divmod(half, PASSES))
                if is_tile(s):
                    exponential(s)
                if s in divide_at and scalar_divides(divide_at[s]):
                    divide_and_store(divide_at[s])
                if is_tile(s - 1):
                    copy_out(s - 1)
                if head_follows and r == 2:
                    q_copy(following_head)
